import numpy as np
import ml_dtypes


def mxq(x, axis, fmt="e4m3"):
    dtype, down = {"e4m3": (ml_dtypes.float8_e4m3fn, 7), "e5m2": (ml_dtypes.float8_e5m2, 14)}[fmt]
    v = np.moveaxis(np.asarray(x, np.float32).astype(ml_dtypes.bfloat16).astype(np.float64), axis, -1)
    blocks = v.reshape(v.shape[:-1] + (-1, 32))
    amax = np.abs(blocks).max(-1, keepdims=True)
    byte = np.maximum(np.where(amax > 0, np.frexp(amax)[1] - 1 + 127, 0) - down, 1)
    scale = np.exp2(byte - 127.0)
    codes = (blocks / scale).astype(np.float32).astype(dtype).astype(np.float64)
    return np.moveaxis((codes * scale).reshape(v.shape), -1, axis)


WIDE = False


def mx_kscale(k):
    if not WIDE:
        return np.ones(k)
    levels = np.array([10, -10, 5, -5, 0])
    a = np.random.permutation(np.resize(levels, k // 512 * 4)).reshape(k // 512, 4)
    idx = np.arange(k)
    return np.exp2(a[idx // 512, idx % 128 // 32])


BF16 = ml_dtypes.bfloat16


def bf(x):
    return np.asarray(x, np.float32).astype(BF16)


def f64(x):
    return np.asarray(x).astype(np.float64)


B, C, H, W, BH, BW, M = 4, 64, 67, 67, 4, 4, 128
EPS = 1.0
N = C * BH * BW
HO, WO = H - BH + 1, W - BW + 1


def extract_patches(x):
    cols = [x[:, :, dh:dh + HO, dw:dw + WO] for dh in range(BH) for dw in range(BW)]
    return np.stack(cols, axis=2).reshape(B, N, HO, WO)


def setup_inputs():
    a = np.log(mx_kscale(N)[::BH * BW])
    return {"x": bf(np.random.standard_normal((B, C, H, W)) * 2.0 + a[None, :, None, None]),
            "offsets": bf(np.random.standard_normal((1, M, C, BH, BW)) * 2.0 - a[None, None, :, None, None])}


def reference(x, offsets):
    patches = extract_patches(f64(x))
    b = f64(offsets).reshape(M, N)
    m_x = np.max(EPS * patches, axis=1, keepdims=True)
    m_b = np.max(EPS * b, axis=1)
    Ex = np.exp(EPS * patches - m_x)
    Eb = np.exp(EPS * b - m_b[:, None])
    S = (mxq(Eb, 1, "e4m3") @ mxq(Ex.reshape(B, N, HO * WO), 1, "e4m3")).reshape(B, M, HO, WO)
    out = (m_x + m_b[None, :, None, None] + np.log(S)) / EPS
    return out - np.log(N) / EPS

@@ -1,0 +1,254 @@
+from contextlib import ExitStack
+import math
+
+import concourse.bass as bass
+import concourse.mybir as mybir
+import concourse.tile as tile
+from concourse.masks import make_identity
+
+FLOPS = 2 * 128 * 1024 * 4 * 64 * 64
+
+BF16 = mybir.dt.bfloat16
+F32 = mybir.dt.float32
+U32 = mybir.dt.uint32
+U8 = mybir.dt.uint8
+FP8X4 = mybir.dt.float8_e4m3fn_x4
+ALU = mybir.AluOpType
+ACT = mybir.ActivationFunctionType
+
+P = 128
+C = 64
+W = 67
+WO = 64
+K = 1024
+ROWS = 8
+UNITS = 64
+LOOKAHEAD = 2
+
+
+def tile_mex_kernel(tc, x, offsets, out):
+    nc = tc.nc
+    with ExitStack() as ctx:
+        ctx.enter_context(tc.manual_schedule())
+        const = ctx.enter_context(tc.tile_pool(name="const", bufs=1))
+        xpool = ctx.enter_context(tc.tile_pool(name="xrep", bufs=1))
+        cmxp = ctx.enter_context(tc.tile_pool(name="cmx", bufs=2))
+        treep = ctx.enter_context(tc.tile_pool(name="tree", bufs=1))
+        dpool = ctx.enter_context(tc.tile_pool(name="diff", bufs=4))
+        gpool = ctx.enter_context(tc.tile_pool(name="grouped", bufs=3))
+        cpool = ctx.enter_context(tc.tile_pool(name="codes", bufs=3))
+        lpool = ctx.enter_context(tc.tile_pool(name="logs", bufs=4))
+        rpool = ctx.enter_context(tc.tile_pool(name="res", bufs=4))
+        ps_acc = ctx.enter_context(tc.psum_pool(name="ps_acc", bufs=4))
+        ps_mb = ctx.enter_context(tc.psum_pool(name="ps_mb", bufs=2))
+
+        ident = const.tile([P, P], BF16, name="ident")
+        make_identity(nc, ident[:])
+
+        offs = const.tile([P, K], BF16, name="offs")
+        nc.sync.dma_start(out=offs[:], in_=offsets[0].rearrange("m c i j -> m (c i j)"))
+
+        def load_cmx(b):
+            t = cmxp.tile([P, C * W], BF16, name="cmx")
+            v = t[:].rearrange("y (c z) -> y c z", z=W)
+            nc.sync.dma_start(out=v[0:64], in_=x[b, :, 0:64, :].rearrange("c y z -> y c z"))
+            nc.sync.dma_start(out=v[64:67], in_=x[b, :, 64:67, :].rearrange("c y z -> y c z"))
+            return t
+
+        xr = {}
+
+        def load_xrep(b):
+            for s in range(2):
+                t = xpool.tile([P, WO * W], BF16, name="xr%d%d" % (b, s))
+                for dh in range(4):
+                    nc.sync.dma_start(
+                        out=t[dh:P:4, :],
+                        in_=x[b, 32 * s : 32 * s + 32, dh : dh + WO, :].rearrange("c y z -> c (y z)"),
+                    )
+                xr[(b, s)] = t
+
+        cmx = {}
+        cmx[0] = load_cmx(0)
+        cmx[1] = load_cmx(1)
+        load_xrep(0)
+        load_xrep(1)
+        cmx[2] = load_cmx(2)
+        cmx[3] = load_cmx(3)
+        load_xrep(2)
+        load_xrep(3)
+
+        mb = const.tile([P, 1], F32, name="mb")
+        nc.vector.tensor_reduce(out=mb[:], in_=offs[:], axis=mybir.AxisListType.X, op=ALU.max)
+        neg_mb = const.tile([P, 1], F32, name="neg_mb")
+        nc.vector.tensor_scalar(out=neg_mb[:], in0=mb[:], scalar1=-1.0, scalar2=None, op0=ALU.mult)
+        cb = const.tile([P, 1], F32, name="cb")
+        nc.vector.tensor_scalar(out=cb[:], in0=mb[:], scalar1=-math.log(float(K)), scalar2=None, op0=ALU.add)
+        eb_t = const.tile([P, 2, 4, P], BF16, name="eb_t")
+        nc.scalar.activation(
+            out=eb_t[:],
+            in_=offs[:].rearrange("m (s q t) -> m s t q", s=2, q=P, t=4),
+            func=ACT.Exp,
+            bias=neg_mb[:, 0:1],
+            scale=1.0,
+        )
+        eb_ps = ps_mb.tile([P, 8, P], BF16, tag="mb2", name="eb_ps")
+        for i in range(8):
+            nc.tensor.transpose(eb_ps[:, i, :], eb_t[:, i // 4, i % 4, :], ident[:])
+        eb_g = const.tile([P, 2, P, 4], BF16, name="eb_g", align_bytes=64)
+        nc.scalar.copy(out=eb_g[:], in_=eb_ps[:].rearrange("q (s t) m -> q s m t", s=2, t=4))
+        eb_codes = const.tile([P, 2 * P], U32, name="eb_codes", align_bytes=64)
+        eb_scales = const.tile([P, 2 * P], U8, name="eb_scales", align_bytes=64)
+
+        R = W
+        m_t = {}
+
+        def channel_max(t, dst):
+            cur = t
+            for lvl, half in enumerate((2144, 1072, 536, 268, 134)):
+                nxt = treep.tile([P, half], BF16, name="tr%d" % lvl)
+                nc.vector.tensor_tensor(out=nxt[:R, :], in0=cur[:R, 0:half], in1=cur[:R, half : 2 * half], op=ALU.max)
+                cur = nxt
+            nc.vector.tensor_tensor(out=dst, in0=cur[:R, 0:W], in1=cur[:R, W : 2 * W], op=ALU.max)
+
+        def max_path(bp):
+            cm = treep.tile([P, 2, W], BF16, name="cm")
+            for blo in range(2):
+                channel_max(cmx[2 * bp + blo], cm[:R, blo, :])
+            a1 = treep.tile([P, 2, W - 1], BF16, name="a1")
+            nc.vector.tensor_tensor(out=a1[:R], in0=cm[:R, :, 0:66], in1=cm[:R, :, 1:67], op=ALU.max)
+            hm_y = treep.tile([P, P], BF16, name="hm_y")
+            nc.vector.memset(hm_y[:], 0.0)
+            nc.vector.tensor_tensor(
+                out=hm_y[:R].rearrange("y (b w) -> y b w", b=2),
+                in0=a1[:R, :, 0:64],
+                in1=a1[:R, :, 2:66],
+                op=ALU.max,
+            )
+            hm_ps = ps_mb.tile([P, 8, P], BF16, tag="mb2", name="hm_ps")
+            nc.tensor.transpose(hm_ps[:, 0, :], hm_y[:], ident[:])
+            hm_t = treep.tile([P, W], BF16, name="hm_t")
+            nc.vector.tensor_copy(out=hm_t[:], in_=hm_ps[:, 0, 0:W])
+            v1 = treep.tile([P, W - 1], BF16, name="v1")
+            nc.vector.tensor_tensor(out=v1[:], in0=hm_t[:, 0:66], in1=hm_t[:, 1:67], op=ALU.max)
+            mt = const.tile([P, WO], BF16, name="m_t%d" % bp)
+            nc.vector.tensor_tensor(out=mt[:], in0=v1[:, 0:64], in1=v1[:, 2:66], op=ALU.max)
+            m_t[bp] = mt
+
+        def make_m(j, tag):
+            t = ps_mb.tile([P, ROWS, P], BF16, tag=tag, name="m_" + tag)
+            for r in range(ROWS):
+                h = ROWS * (j % 8) + r
+                nc.tensor.transpose(t[:, r, :], m_t[j // 8][:, h : h + 1].to_broadcast([P, P]), ident[:])
+            return t
+
+        max_path(0)
+        nc.vector.quantize_mx(
+            out=eb_codes[:].bitcast(FP8X4),
+            scales=eb_scales[:],
+            in_=eb_g[:].rearrange("q s m t -> q (s m t)"),
+        )
+
+        m_sub = {}
+        d_t = {}
+        g_t = {}
+        q_t = {}
+        acc_t = {}
+        ln_t = {}
+        m_add = {}
+
+        def where(u):
+            j = u // 4
+            blo = (u // 2) % 2
+            return j, blo, u % 2, 2 * (j // 8) + blo, ROWS * (j % 8)
+
+        def sub(u):
+            j, blo, s, b, h0 = where(u)
+            d = dpool.tile([P, 2048], F32, name="d")
+            xv = xr[(b, s)][:].rearrange("p (h z) -> p h z", z=W)
+            dv = d[:].rearrange("p (h a f t) -> p h a f t", h=ROWS, a=16, f=4, t=4)
+            mv = m_sub[j][:].rearrange("p h (b a f) -> p h b a f", b=2, a=16, f=4)
+            for f in range(4):
+                nc.vector.tensor_tensor(
+                    out=dv[:, :, :, f, :],
+                    in0=xv[:, h0 : h0 + ROWS, f : f + WO].rearrange("p h (a t) -> p h a t", t=4),
+                    in1=mv[:, :, blo, :, f : f + 1].to_broadcast([P, ROWS, 16, 4]),
+                    op=ALU.subtract,
+                )
+            d_t[u] = d
+
+        def expo(u):
+            g = gpool.tile([P, 2048], BF16, name="g", align_bytes=64)
+            nc.scalar.activation(out=g[:], in_=d_t[u][:], func=ACT.Exp)
+            g_t[u] = g
+
+        def quant(u):
+            codes = cpool.tile([P, 512], U32, name="codes", align_bytes=64)
+            scales = cpool.tile([P, 512], U8, name="scales", align_bytes=64)
+            nc.vector.quantize_mx(out=codes[:].bitcast(FP8X4), scales=scales[:], in_=g_t[u][:])
+            q_t[u] = (codes, scales)
+
+        def mx(u):
+            s = u % 2
+            if s == 0:
+                acc = ps_acc.tile([P, 512], F32, name="acc")
+                acc_t[u // 2] = acc
+            codes, scales = q_t[u]
+            nc.tensor.matmul_mx(
+                out=acc_t[u // 2][:],
+                lhsT=eb_codes[:, P * s : P * s + P].bitcast(FP8X4),
+                lhsT_scale=eb_scales[:, P * s : P * s + P],
+                rhs=codes[:].bitcast(FP8X4),
+                rhs_scale=scales[:],
+                start=(s == 0),
+                stop=(s == 1),
+            )
+
+        def log_of(gi):
+            ln = lpool.tile([P, 512], F32, name="ln")
+            nc.scalar.activation(out=ln[:], in_=acc_t[gi][:], func=ACT.Ln)
+            ln_t[gi] = ln
+
+        def finish(gi):
+            j, blo, s, b, h0 = where(2 * gi)
+            res = rpool.tile([P, 512], F32, name="res")
+            nc.vector.scalar_tensor_tensor(
+                out=res[:].rearrange("p (h w) -> p h w", w=WO),
+                in0=ln_t[gi][:].rearrange("p (h w) -> p h w", w=WO),
+                scalar=cb[:, 0:1],
+                in1=m_add[j][:].rearrange("p h (b w) -> p h b w", b=2)[:, :, blo, :],
+                op0=ALU.add,
+                op1=ALU.add,
+            )
+            nc.sync.dma_start(out=out[b, :, h0 : h0 + ROWS, :].rearrange("m h w -> m (h w)"), in_=res[:])
+
+        m_sub[0] = make_m(0, "mb")
+        m_sub[1] = make_m(1, "mb")
+        sub(0)
+        sub(1)
+        expo(0)
+        pending = []
+        for u in range(UNITS):
+            nxt = u + LOOKAHEAD
+            if u == 12:
+                max_path(1)
+            if nxt < UNITS:
+                if nxt % 4 == 0 and nxt // 4 + 1 < 16:
+                    m_sub[nxt // 4 + 1] = make_m(nxt // 4 + 1, "mb")
+                sub(nxt)
+            if u + 1 < UNITS:
+                expo(u + 1)
+            if pending and (u % 8 == 1):
+                for gi in pending:
+                    finish(gi)
+                pending = []
+            quant(u)
+            mx(u)
+            if u % 8 == 7:
+                ph = u // 8
+                m_add[2 * ph] = make_m(2 * ph, "mb2")
+                m_add[2 * ph + 1] = make_m(2 * ph + 1, "mb2")
+                for gi in range(4 * ph, 4 * ph + 4):
+                    log_of(gi)
+                    pending.append(gi)
+        for gi in pending:
+            finish(gi)

@@ -21,9 +21,10 @@ C = 64
 W = 67
 WO = 64
 K = 1024
-ROWS = 8
-UNITS = 64
-LOOKAHEAD = 2
+PITCH = 144
+QUADS = 64
+GROUPS = 32
+PHASE_AT = 50
 
 
 def tile_mex_kernel(tc, x, offsets, out):
@@ -31,51 +32,54 @@ def tile_mex_kernel(tc, x, offsets, out):
     with ExitStack() as ctx:
         ctx.enter_context(tc.manual_schedule())
         const = ctx.enter_context(tc.tile_pool(name="const", bufs=1))
-        xpool = ctx.enter_context(tc.tile_pool(name="xrep", bufs=1))
+        xpool = ctx.enter_context(tc.tile_pool(name="xh", bufs=1))
         cmxp = ctx.enter_context(tc.tile_pool(name="cmx", bufs=2))
         treep = ctx.enter_context(tc.tile_pool(name="tree", bufs=1))
-        dpool = ctx.enter_context(tc.tile_pool(name="diff", bufs=4))
-        gpool = ctx.enter_context(tc.tile_pool(name="grouped", bufs=3))
-        cpool = ctx.enter_context(tc.tile_pool(name="codes", bufs=3))
-        lpool = ctx.enter_context(tc.tile_pool(name="logs", bufs=4))
-        rpool = ctx.enter_context(tc.tile_pool(name="res", bufs=4))
-        ps_acc = ctx.enter_context(tc.psum_pool(name="ps_acc", bufs=4))
+        epool = ctx.enter_context(tc.tile_pool(name="ex", bufs=8))
+        gpool = ctx.enter_context(tc.tile_pool(name="grouped", bufs=4))
+        cpool = ctx.enter_context(tc.tile_pool(name="codes", bufs=4))
+        spool = ctx.enter_context(tc.tile_pool(name="sums", bufs=1))
+        ps_tp = ctx.enter_context(tc.psum_pool(name="ps_tp", bufs=4))
+        ps_acc = ctx.enter_context(tc.psum_pool(name="ps_acc", bufs=2))
         ps_mb = ctx.enter_context(tc.psum_pool(name="ps_mb", bufs=2))
 
         ident = const.tile([P, P], BF16, name="ident")
         make_identity(nc, ident[:])
+        ident_f = const.tile([P, P], F32, name="ident_f")
+        make_identity(nc, ident_f[:])
 
         offs = const.tile([P, K], BF16, name="offs")
         nc.sync.dma_start(out=offs[:], in_=offsets[0].rearrange("m c i j -> m (c i j)"))
+
+        cmx = {}
+        xh = {}
 
         def load_cmx(b):
             t = cmxp.tile([P, C * W], BF16, name="cmx")
             v = t[:].rearrange("y (c z) -> y c z", z=W)
             nc.sync.dma_start(out=v[0:64], in_=x[b, :, 0:64, :].rearrange("c y z -> y c z"))
             nc.sync.dma_start(out=v[64:67], in_=x[b, :, 64:67, :].rearrange("c y z -> y c z"))
-            return t
+            cmx[b] = t
 
-        xr = {}
-
-        def load_xrep(b):
-            for s in range(2):
-                t = xpool.tile([P, WO * W], BF16, name="xr%d%d" % (b, s))
-                for dh in range(4):
+        def load_xh(b):
+            t = xpool.tile([P, C, PITCH], BF16, name="xh%d" % b)
+            for u in range(2):
+                for f in range(2):
+                    y0 = f + 2 * u
                     nc.sync.dma_start(
-                        out=t[dh:P:4, :],
-                        in_=x[b, 32 * s : 32 * s + 32, dh : dh + WO, :].rearrange("c y z -> c (y z)"),
+                        out=t[2 * f + u : P : 4, :, 0 : 2 * W],
+                        in_=x[b, :, y0 : y0 + WO, :].rearrange("c (a e) z -> a c (e z)", e=2),
                     )
-                xr[(b, s)] = t
+            xh[b] = t
 
-        cmx = {}
-        cmx[0] = load_cmx(0)
-        cmx[1] = load_cmx(1)
-        load_xrep(0)
-        load_xrep(1)
-        cmx[2] = load_cmx(2)
-        cmx[3] = load_cmx(3)
-        load_xrep(2)
-        load_xrep(3)
+        load_cmx(0)
+        load_xh(0)
+        load_cmx(1)
+        load_xh(1)
+        load_cmx(2)
+        load_cmx(3)
+        load_xh(2)
+        load_xh(3)
 
         mb = const.tile([P, 1], F32, name="mb")
         nc.vector.tensor_reduce(out=mb[:], in_=offs[:], axis=mybir.AxisListType.X, op=ALU.max)
@@ -83,118 +87,186 @@ def tile_mex_kernel(tc, x, offsets, out):
         nc.vector.tensor_scalar(out=neg_mb[:], in0=mb[:], scalar1=-1.0, scalar2=None, op0=ALU.mult)
         cb = const.tile([P, 1], F32, name="cb")
         nc.vector.tensor_scalar(out=cb[:], in0=mb[:], scalar1=-math.log(float(K)), scalar2=None, op0=ALU.add)
-        eb_t = const.tile([P, 2, 4, P], BF16, name="eb_t")
-        nc.scalar.activation(
-            out=eb_t[:],
-            in_=offs[:].rearrange("m (s q t) -> m s t q", s=2, q=P, t=4),
-            func=ACT.Exp,
-            bias=neg_mb[:, 0:1],
-            scale=1.0,
-        )
-        eb_ps = ps_mb.tile([P, 8, P], BF16, tag="mb2", name="eb_ps")
-        for i in range(8):
-            nc.tensor.transpose(eb_ps[:, i, :], eb_t[:, i // 4, i % 4, :], ident[:])
+        eb_t = const.tile([P, 2, 2, 32, 8], BF16, name="eb_t")
+        for s in range(2):
+            nc.scalar.activation(
+                out=eb_t[:, s],
+                in_=offs[:, 512 * s : 512 * s + 512].rearrange("m (c u r) -> m u c r", c=32, u=2, r=8),
+                func=ACT.Exp,
+                bias=neg_mb[:, 0:1],
+                scale=1.0,
+            )
+        eb_w = eb_t[:].rearrange("m s u c r -> m (s u c r)").bitcast(F32)
+        eb_ps = ps_mb.tile([P, 4, P], F32, tag="mb", name="eb_ps")
+        for i in range(4):
+            nc.tensor.transpose(eb_ps[:, i, :], eb_w[:, P * i : P * i + P], ident_f[:])
         eb_g = const.tile([P, 2, P, 4], BF16, name="eb_g", align_bytes=64)
-        nc.scalar.copy(out=eb_g[:], in_=eb_ps[:].rearrange("q (s t) m -> q s m t", s=2, t=4))
+        nc.vector.tensor_copy(
+            out=eb_g[:].rearrange("q s m t -> q (s m t)").bitcast(F32).rearrange("q (s m u) -> q s m u", s=2, m=P, u=2),
+            in_=eb_ps[:].rearrange("q (s u) m -> q s m u", s=2, u=2),
+        )
         eb_codes = const.tile([P, 2 * P], U32, name="eb_codes", align_bytes=64)
         eb_scales = const.tile([P, 2 * P], U8, name="eb_scales", align_bytes=64)
 
         R = W
         m_t = {}
+        negm = {}
+        cm = {}
+        hm_y = const.tile([P, P], BF16, name="hm_y")
+        nc.vector.memset(hm_y[:], 0.0)
+        for bp in range(2):
+            cm[bp] = const.tile([P, 2, W], BF16, name="cm%d" % bp)
+        nc.vector.memset(cm[0][:], 0.0)
 
-        def channel_max(t, dst):
-            cur = t
-            for lvl, half in enumerate((2144, 1072, 536, 268, 134)):
-                nxt = treep.tile([P, half], BF16, name="tr%d" % lvl)
-                nc.vector.tensor_tensor(out=nxt[:R, :], in0=cur[:R, 0:half], in1=cur[:R, half : 2 * half], op=ALU.max)
-                cur = nxt
-            nc.vector.tensor_tensor(out=dst, in0=cur[:R, 0:W], in1=cur[:R, W : 2 * W], op=ALU.max)
+        def channel_max_tasks(b):
+            state = {}
 
-        def max_path(bp):
-            cm = treep.tile([P, 2, W], BF16, name="cm")
-            for blo in range(2):
-                channel_max(cmx[2 * bp + blo], cm[:R, blo, :])
-            a1 = treep.tile([P, 2, W - 1], BF16, name="a1")
-            nc.vector.tensor_tensor(out=a1[:R], in0=cm[:R, :, 0:66], in1=cm[:R, :, 1:67], op=ALU.max)
-            hm_y = treep.tile([P, P], BF16, name="hm_y")
-            nc.vector.memset(hm_y[:], 0.0)
-            nc.vector.tensor_tensor(
-                out=hm_y[:R].rearrange("y (b w) -> y b w", b=2),
-                in0=a1[:R, :, 0:64],
-                in1=a1[:R, :, 2:66],
-                op=ALU.max,
-            )
-            hm_ps = ps_mb.tile([P, 8, P], BF16, tag="mb2", name="hm_ps")
-            nc.tensor.transpose(hm_ps[:, 0, :], hm_y[:], ident[:])
-            hm_t = treep.tile([P, W], BF16, name="hm_t")
-            nc.vector.tensor_copy(out=hm_t[:], in_=hm_ps[:, 0, 0:W])
-            v1 = treep.tile([P, W - 1], BF16, name="v1")
-            nc.vector.tensor_tensor(out=v1[:], in0=hm_t[:, 0:66], in1=hm_t[:, 1:67], op=ALU.max)
-            mt = const.tile([P, WO], BF16, name="m_t%d" % bp)
-            nc.vector.tensor_tensor(out=mt[:], in0=v1[:, 0:64], in1=v1[:, 2:66], op=ALU.max)
-            m_t[bp] = mt
+            def level0(part):
+                def run():
+                    if part == 0:
+                        state["t0"] = treep.tile([P, 2144], BF16, name="tr0")
+                    lo = 1072 * part
+                    nc.vector.tensor_tensor(
+                        out=state["t0"][:R, lo : lo + 1072],
+                        in0=cmx[b][:R, lo : lo + 1072],
+                        in1=cmx[b][:R, 2144 + lo : 2144 + lo + 1072],
+                        op=ALU.max,
+                    )
 
-        def make_m(j, tag):
-            t = ps_mb.tile([P, ROWS, P], BF16, tag=tag, name="m_" + tag)
-            for r in range(ROWS):
-                h = ROWS * (j % 8) + r
-                nc.tensor.transpose(t[:, r, :], m_t[j // 8][:, h : h + 1].to_broadcast([P, P]), ident[:])
+                return run
+
+            def level1():
+                t1 = treep.tile([P, 1072], BF16, name="tr1")
+                nc.vector.tensor_tensor(
+                    out=t1[:R, :], in0=state["t0"][:R, 0:1072], in1=state["t0"][:R, 1072:2144], op=ALU.max
+                )
+                state["t1"] = t1
+
+            def rest():
+                cur = state["t1"]
+                for lvl, half in enumerate((536, 268, 134)):
+                    nxt = treep.tile([P, half], BF16, name="tr%d" % (lvl + 2))
+                    nc.vector.tensor_tensor(
+                        out=nxt[:R, :], in0=cur[:R, 0:half], in1=cur[:R, half : 2 * half], op=ALU.max
+                    )
+                    cur = nxt
+                nc.vector.tensor_tensor(
+                    out=cm[b // 2][:R, b % 2, :], in0=cur[:R, 0:W], in1=cur[:R, W : 2 * W], op=ALU.max
+                )
+
+            return [level0(0), level0(1), level1, rest]
+
+        def pair_tasks(bp, key):
+            state = {}
+
+            def first():
+                a1 = treep.tile([P, 2, W - 1], BF16, name="a1")
+                nc.vector.tensor_tensor(out=a1[:R], in0=cm[bp][:R, :, 0:66], in1=cm[bp][:R, :, 1:67], op=ALU.max)
+                nc.vector.tensor_tensor(
+                    out=hm_y[:R].rearrange("y (b w) -> y b w", b=2),
+                    in0=a1[:R, :, 0:64],
+                    in1=a1[:R, :, 2:66],
+                    op=ALU.max,
+                )
+                hm_ps = ps_mb.tile([P, 8, P], BF16, tag="mb", name="hm_ps")
+                nc.tensor.transpose(hm_ps[:, 0, :], hm_y[:], ident[:])
+                state["hm_ps"] = hm_ps
+
+            def second():
+                hm_t = treep.tile([P, W], BF16, name="hm_t")
+                nc.vector.tensor_copy(out=hm_t[:], in_=state["hm_ps"][:, 0, 0:W])
+                v1 = treep.tile([P, W - 1], BF16, name="v1")
+                nc.vector.tensor_tensor(out=v1[:], in0=hm_t[:, 0:66], in1=hm_t[:, 1:67], op=ALU.max)
+                mt = const.tile([P, WO], BF16, name="m_t" + key)
+                nc.vector.tensor_tensor(out=mt[:], in0=v1[:, 0:64], in1=v1[:, 2:66], op=ALU.max)
+                m_t[key] = mt
+                rep = treep.tile([P, WO, 2], BF16, name="rep")
+                nc.vector.tensor_copy(out=rep[:], in_=mt[:].unsqueeze(2).to_broadcast([P, WO, 2]))
+                nm_ps = ps_mb.tile([P, 8, P], BF16, tag="mb", name="nm_ps")
+                nc.tensor.transpose(nm_ps[:, 0, :], rep[:].rearrange("p j u -> p (j u)"), ident[:])
+                state["nm_ps"] = nm_ps
+
+            def third():
+                nm = const.tile([P, P], F32, name="negm" + key)
+                nc.vector.tensor_scalar(
+                    out=nm[:], in0=state["nm_ps"][:, 0, :], scalar1=-1.0, scalar2=None, op0=ALU.mult
+                )
+                negm[key] = nm
+
+            return [first, second, third]
+
+        def make_m(key, blk):
+            t = ps_mb.tile([P, 8, P], BF16, tag="mb", name="m_bc")
+            for r in range(8):
+                h = 8 * blk + r
+                nc.tensor.transpose(t[:, r, :], m_t[key][:, h : h + 1].to_broadcast([P, P]), ident[:])
             return t
 
-        max_path(0)
+        for task in channel_max_tasks(0) + pair_tasks(0, "0a"):
+            task()
         nc.vector.quantize_mx(
             out=eb_codes[:].bitcast(FP8X4),
             scales=eb_scales[:],
             in_=eb_g[:].rearrange("q s m t -> q (s m t)"),
         )
+        background = channel_max_tasks(1) + pair_tasks(0, "0")
+        background = background + channel_max_tasks(2) + channel_max_tasks(3) + pair_tasks(1, "1")
+        bias_key = {0: "0a", 1: "0", 2: "1", 3: "1"}
 
-        m_sub = {}
-        d_t = {}
+        sums = {}
+        for b in range(4):
+            sums[b] = spool.tile([P, WO, WO], F32, name="sum%d" % b)
+        ex_t = {}
+        tp_t = {}
         g_t = {}
         q_t = {}
         acc_t = {}
-        ln_t = {}
-        m_add = {}
 
-        def where(u):
-            j = u // 4
-            blo = (u // 2) % 2
-            return j, blo, u % 2, 2 * (j // 8) + blo, ROWS * (j % 8)
+        def act(i, wi):
+            b = i // 16
+            w = 4 * (i % 16) + wi
+            ex = epool.tile([P, 512], BF16, name="ex")
+            xv = xh[b][:, :, 0 : 2 * W].rearrange("p c (r z) -> p c r z", r=2)
+            col = WO * (b % 2) + w
+            nc.scalar.activation(
+                out=ex[:].rearrange("p (c r d) -> p c r d", c=C, r=2, d=4),
+                in_=xv[:, :, :, w : w + 4],
+                func=ACT.Exp,
+                bias=negm[bias_key[b]][:, col : col + 1],
+                scale=1.0,
+            )
+            ex_t[(i, wi)] = ex
 
-        def sub(u):
-            j, blo, s, b, h0 = where(u)
-            d = dpool.tile([P, 2048], F32, name="d")
-            xv = xr[(b, s)][:].rearrange("p (h z) -> p h z", z=W)
-            dv = d[:].rearrange("p (h a f t) -> p h a f t", h=ROWS, a=16, f=4, t=4)
-            mv = m_sub[j][:].rearrange("p h (b a f) -> p h b a f", b=2, a=16, f=4)
-            for f in range(4):
-                nc.vector.tensor_tensor(
-                    out=dv[:, :, :, f, :],
-                    in0=xv[:, h0 : h0 + ROWS, f : f + WO].rearrange("p h (a t) -> p h a t", t=4),
-                    in1=mv[:, :, blo, :, f : f + 1].to_broadcast([P, ROWS, 16, 4]),
-                    op=ALU.subtract,
-                )
-            d_t[u] = d
+        def tr(i, wi):
+            if wi == 0:
+                for s in range(2):
+                    tp_t[(i, s)] = ps_tp.tile([P, 4, P], F32, name="tp")
+            words = ex_t[(i, wi)][:].bitcast(F32)
+            for s in range(2):
+                nc.tensor.transpose(tp_t[(i, s)][:, wi, :], words[:, P * s : P * s + P], ident_f[:])
 
-        def expo(u):
-            g = gpool.tile([P, 2048], BF16, name="g", align_bytes=64)
-            nc.scalar.activation(out=g[:], in_=d_t[u][:], func=ACT.Exp)
-            g_t[u] = g
+        def cp(i, s):
+            gi = i // 2
+            if i % 2 == 0:
+                g_t[(gi, s)] = gpool.tile([P, 2048], BF16, name="g", align_bytes=64)
+            lo = 512 * (i % 2)
+            nc.vector.tensor_copy(
+                out=g_t[(gi, s)][:].bitcast(F32)[:, lo : lo + 512],
+                in_=tp_t[(i, s)][:].rearrange("q w n -> q (w n)"),
+            )
 
-        def quant(u):
+        def quant(gi, s):
             codes = cpool.tile([P, 512], U32, name="codes", align_bytes=64)
             scales = cpool.tile([P, 512], U8, name="scales", align_bytes=64)
-            nc.vector.quantize_mx(out=codes[:].bitcast(FP8X4), scales=scales[:], in_=g_t[u][:])
-            q_t[u] = (codes, scales)
+            nc.vector.quantize_mx(out=codes[:].bitcast(FP8X4), scales=scales[:], in_=g_t[(gi, s)][:])
+            q_t[(gi, s)] = (codes, scales)
 
-        def mx(u):
-            s = u % 2
+        def mx(gi, s):
             if s == 0:
-                acc = ps_acc.tile([P, 512], F32, name="acc")
-                acc_t[u // 2] = acc
-            codes, scales = q_t[u]
+                acc_t[gi] = ps_acc.tile([P, 512], F32, name="acc")
+            codes, scales = q_t[(gi, s)]
             nc.tensor.matmul_mx(
-                out=acc_t[u // 2][:],
+                out=acc_t[gi][:],
                 lhsT=eb_codes[:, P * s : P * s + P].bitcast(FP8X4),
                 lhsT_scale=eb_scales[:, P * s : P * s + P],
                 rhs=codes[:].bitcast(FP8X4),
@@ -203,52 +275,78 @@ def tile_mex_kernel(tc, x, offsets, out):
                 stop=(s == 1),
             )
 
-        def log_of(gi):
-            ln = lpool.tile([P, 512], F32, name="ln")
-            nc.scalar.activation(out=ln[:], in_=acc_t[gi][:], func=ACT.Ln)
-            ln_t[gi] = ln
+        def acc_copy(gi):
+            b = gi // 8
+            w0 = 8 * (gi % 8)
+            nc.vector.tensor_copy(
+                out=sums[b][:, :, w0 : w0 + 8],
+                in_=acc_t[gi][:].rearrange("m (w j) -> m j w", w=8),
+            )
 
-        def finish(gi):
-            j, blo, s, b, h0 = where(2 * gi)
-            res = rpool.tile([P, 512], F32, name="res")
+        def log_of(b, r0, rows):
+            v = sums[b][:, r0 : r0 + rows, :].rearrange("m j w -> m (j w)")
+            nc.scalar.activation(out=v, in_=v, func=ACT.Ln)
+
+        def finish(b, blk, m_bc):
+            v = sums[b][:, 8 * blk : 8 * blk + 8, :]
             nc.vector.scalar_tensor_tensor(
-                out=res[:].rearrange("p (h w) -> p h w", w=WO),
-                in0=ln_t[gi][:].rearrange("p (h w) -> p h w", w=WO),
+                out=v,
+                in0=v,
                 scalar=cb[:, 0:1],
-                in1=m_add[j][:].rearrange("p h (b w) -> p h b w", b=2)[:, :, blo, :],
+                in1=m_bc[:].rearrange("p h (b w) -> p h b w", b=2)[:, :, b % 2, :],
                 op0=ALU.add,
                 op1=ALU.add,
             )
-            nc.sync.dma_start(out=out[b, :, h0 : h0 + ROWS, :].rearrange("m h w -> m (h w)"), in_=res[:])
 
-        m_sub[0] = make_m(0, "mb")
-        m_sub[1] = make_m(1, "mb")
-        sub(0)
-        sub(1)
-        expo(0)
-        pending = []
-        for u in range(UNITS):
-            nxt = u + LOOKAHEAD
-            if u == 12:
-                max_path(1)
-            if nxt < UNITS:
-                if nxt % 4 == 0 and nxt // 4 + 1 < 16:
-                    m_sub[nxt // 4 + 1] = make_m(nxt // 4 + 1, "mb")
-                sub(nxt)
-            if u + 1 < UNITS:
-                expo(u + 1)
-            if pending and (u % 8 == 1):
-                for gi in pending:
-                    finish(gi)
-                pending = []
-            quant(u)
-            mx(u)
-            if u % 8 == 7:
-                ph = u // 8
-                m_add[2 * ph] = make_m(2 * ph, "mb2")
-                m_add[2 * ph + 1] = make_m(2 * ph + 1, "mb2")
-                for gi in range(4 * ph, 4 * ph + 4):
-                    log_of(gi)
-                    pending.append(gi)
-        for gi in pending:
-            finish(gi)
+        def store(b, r0, rows):
+            nc.sync.dma_start(
+                out=out[b, :, r0 : r0 + rows, :].rearrange("m h w -> m (h w)"),
+                in_=sums[b][:, r0 : r0 + rows, :].rearrange("m j w -> m (j w)"),
+            )
+
+        def phase_one():
+            for half in range(2):
+                log_of(0, 32 * half, 32)
+                log_of(1, 32 * half, 32)
+                for blk in range(4 * half, 4 * half + 4):
+                    m_bc = make_m("0", blk)
+                    finish(0, blk, m_bc)
+                    finish(1, blk, m_bc)
+                store(0, 32 * half, 32)
+                store(1, 32 * half, 32)
+            for half in range(2):
+                log_of(2, 32 * half, 32)
+                for blk in range(4 * half, 4 * half + 4):
+                    finish(2, blk, make_m("1", blk))
+                store(2, 32 * half, 32)
+
+        for i in range(QUADS + 3):
+            odd_g = (i - 3) // 2 if (i % 2 == 1 and i >= 3) else None
+            if i < QUADS:
+                for wi in range(4):
+                    act(i, wi)
+                    tr(i, wi)
+            if 1 <= i <= QUADS:
+                cp(i - 1, 0)
+            if odd_g is not None:
+                quant(odd_g, 0)
+            if 1 <= i <= QUADS:
+                cp(i - 1, 1)
+            if odd_g is not None:
+                quant(odd_g, 1)
+                mx(odd_g, 0)
+                mx(odd_g, 1)
+            if i % 2 == 0 and i >= 4:
+                acc_copy((i - 4) // 2)
+            if i >= 3 and background:
+                task = background[0]
+                task()
+                background = background[1:]
+            if i == PHASE_AT:
+                phase_one()
+
+        for qd in range(4):
+            log_of(3, 16 * qd, 16)
+            for blk in (2 * qd, 2 * qd + 1):
+                finish(3, blk, make_m("1", blk))
+            store(3, 16 * qd, 16)

@@ -21,10 +21,14 @@ C = 64
 W = 67
 WO = 64
 K = 1024
-PITCH = 144
-QUADS = 64
-GROUPS = 32
-PHASE_AT = 50
+NI = 34
+UNITS = 128
+PHASE1_AT = 68
+PHASE2_AT = 116
+BG_START = 30
+CHUNKS0 = ((0, 4), (4, 9), (9, 16))
+CHUNKS0B = ((16, 25), (25, 34))
+CHUNKS1 = ((0, 8), (8, 20), (20, 34))
 
 
 def tile_mex_kernel(tc, x, offsets, out):
@@ -32,14 +36,16 @@ def tile_mex_kernel(tc, x, offsets, out):
     with ExitStack() as ctx:
         ctx.enter_context(tc.manual_schedule())
         const = ctx.enter_context(tc.tile_pool(name="const", bufs=1))
-        xpool = ctx.enter_context(tc.tile_pool(name="xh", bufs=1))
+        xcp = ctx.enter_context(tc.tile_pool(name="xc", bufs=1))
         cmxp = ctx.enter_context(tc.tile_pool(name="cmx", bufs=2))
         treep = ctx.enter_context(tc.tile_pool(name="tree", bufs=1))
-        epool = ctx.enter_context(tc.tile_pool(name="ex", bufs=8))
-        gpool = ctx.enter_context(tc.tile_pool(name="grouped", bufs=4))
-        cpool = ctx.enter_context(tc.tile_pool(name="codes", bufs=4))
+        e1p = ctx.enter_context(tc.tile_pool(name="e1", bufs=18))
+        epool = ctx.enter_context(tc.tile_pool(name="ex", bufs=4))
+        gpool = ctx.enter_context(tc.tile_pool(name="grouped", bufs=2))
+        cpool = ctx.enter_context(tc.tile_pool(name="codes", bufs=2))
         spool = ctx.enter_context(tc.tile_pool(name="sums", bufs=1))
-        ps_tp = ctx.enter_context(tc.psum_pool(name="ps_tp", bufs=4))
+        ps_x1 = ctx.enter_context(tc.psum_pool(name="ps_x1", bufs=2))
+        ps_tp = ctx.enter_context(tc.psum_pool(name="ps_tp", bufs=2))
         ps_acc = ctx.enter_context(tc.psum_pool(name="ps_acc", bufs=2))
         ps_mb = ctx.enter_context(tc.psum_pool(name="ps_mb", bufs=2))
 
@@ -47,12 +53,20 @@ def tile_mex_kernel(tc, x, offsets, out):
         make_identity(nc, ident[:])
         ident_f = const.tile([P, P], F32, name="ident_f")
         make_identity(nc, ident_f[:])
+        perm = const.tile([P, P], BF16, name="perm")
+        nc.vector.tensor_copy(
+            out=perm[:].rearrange("p (x g i e) -> p x g i e", x=4, g=4, i=4, e=2),
+            in_=ident[:].rearrange("p (x i g e) -> p x g i e", x=4, i=4, g=4, e=2),
+        )
 
         offs = const.tile([P, K], BF16, name="offs")
         nc.sync.dma_start(out=offs[:], in_=offsets[0].rearrange("m c i j -> m (c i j)"))
 
         cmx = {}
-        xh = {}
+        xc = {}
+        for bp in range(2):
+            xc[bp] = xcp.tile([P, 4, NI, 2, WO], BF16, name="xc%d" % bp)
+            nc.vector.memset(xc[bp][64:128, :, NI - 1, :, :], 0.0)
 
         def load_cmx(b):
             t = cmxp.tile([P, C * W], BF16, name="cmx")
@@ -61,25 +75,29 @@ def tile_mex_kernel(tc, x, offsets, out):
             nc.sync.dma_start(out=v[64:67], in_=x[b, :, 64:67, :].rearrange("c y z -> y c z"))
             cmx[b] = t
 
-        def load_xh(b):
-            t = xpool.tile([P, C, PITCH], BF16, name="xh%d" % b)
-            for u in range(2):
-                for f in range(2):
-                    y0 = f + 2 * u
-                    nc.sync.dma_start(
-                        out=t[2 * f + u : P : 4, :, 0 : 2 * W],
-                        in_=x[b, :, y0 : y0 + WO, :].rearrange("c (a e) z -> a c (e z)", e=2),
-                    )
-            xh[b] = t
+        def load_xc(bp, i0, i1):
+            for dw in range(4):
+                for b2 in range(2):
+                    for rho in range(2):
+                        hi = min(i1, NI - rho)
+                        n = hi - i0
+                        if n > 0:
+                            y0 = 2 * i0 + rho
+                            nc.sync.dma_start(
+                                out=xc[bp][64 * rho : 64 * rho + 64, dw, i0:hi, b2, :],
+                                in_=x[2 * bp + b2, :, y0 : y0 + 2 * n - 1 : 2, dw : dw + WO],
+                            )
 
         load_cmx(0)
-        load_xh(0)
         load_cmx(1)
-        load_xh(1)
+        for i0, i1 in CHUNKS0:
+            load_xc(0, i0, i1)
         load_cmx(2)
         load_cmx(3)
-        load_xh(2)
-        load_xh(3)
+        for i0, i1 in CHUNKS0B:
+            load_xc(0, i0, i1)
+        for i0, i1 in CHUNKS1:
+            load_xc(1, i0, i1)
 
         mb = const.tile([P, 1], F32, name="mb")
         nc.vector.tensor_reduce(out=mb[:], in_=offs[:], axis=mybir.AxisListType.X, op=ALU.max)
@@ -87,19 +105,21 @@ def tile_mex_kernel(tc, x, offsets, out):
         nc.vector.tensor_scalar(out=neg_mb[:], in0=mb[:], scalar1=-1.0, scalar2=None, op0=ALU.mult)
         cb = const.tile([P, 1], F32, name="cb")
         nc.vector.tensor_scalar(out=cb[:], in0=mb[:], scalar1=-math.log(float(K)), scalar2=None, op0=ALU.add)
-        eb_t = const.tile([P, 2, 2, 32, 8], BF16, name="eb_t")
-        for s in range(2):
-            nc.scalar.activation(
-                out=eb_t[:, s],
-                in_=offs[:, 512 * s : 512 * s + 512].rearrange("m (c u r) -> m u c r", c=32, u=2, r=8),
-                func=ACT.Exp,
-                bias=neg_mb[:, 0:1],
-                scale=1.0,
-            )
-        eb_w = eb_t[:].rearrange("m s u c r -> m (s u c r)").bitcast(F32)
+        eb_n = const.tile([P, C, 4, 4], BF16, name="eb_n")
+        nc.scalar.activation(
+            out=eb_n[:].rearrange("m c d w -> m (c d w)"), in_=offs[:], func=ACT.Exp, bias=neg_mb[:, 0:1], scale=1.0
+        )
+        eb_t = const.tile([P, 4, C, 4], BF16, name="eb_t")
+        for dh in range(4):
+            for a in range(2):
+                nc.vector.tensor_copy(
+                    out=eb_t[:, dh, 32 * a : 32 * a + 32, :].rearrange("m (g i e) w -> m g i e w", g=4, i=4, e=2),
+                    in_=eb_n[:, 32 * a : 32 * a + 32, dh, :].rearrange("m (i g e) w -> m g i e w", i=4, g=4, e=2),
+                )
+        eb_w = eb_t[:].rearrange("m d c w -> m (d c w)").bitcast(F32)
         eb_ps = ps_mb.tile([P, 4, P], F32, tag="mb", name="eb_ps")
-        for i in range(4):
-            nc.tensor.transpose(eb_ps[:, i, :], eb_w[:, P * i : P * i + P], ident_f[:])
+        for dh in range(4):
+            nc.tensor.transpose(eb_ps[:, dh, :], eb_w[:, P * dh : P * dh + P], ident_f[:])
         eb_g = const.tile([P, 2, P, 4], BF16, name="eb_g", align_bytes=64)
         nc.vector.tensor_copy(
             out=eb_g[:].rearrange("q s m t -> q (s m t)").bitcast(F32).rearrange("q (s m u) -> q s m u", s=2, m=P, u=2),
@@ -110,13 +130,13 @@ def tile_mex_kernel(tc, x, offsets, out):
 
         R = W
         m_t = {}
-        negm = {}
+        neg_hm = {}
+        r_t = {}
         cm = {}
         hm_y = const.tile([P, P], BF16, name="hm_y")
         nc.vector.memset(hm_y[:], 0.0)
         for bp in range(2):
             cm[bp] = const.tile([P, 2, W], BF16, name="cm%d" % bp)
-        nc.vector.memset(cm[0][:], 0.0)
 
         def channel_max_tasks(b):
             state = {}
@@ -156,7 +176,7 @@ def tile_mex_kernel(tc, x, offsets, out):
 
             return [level0(0), level0(1), level1, rest]
 
-        def pair_tasks(bp, key):
+        def pair_tasks(bp):
             state = {}
 
             def first():
@@ -173,180 +193,232 @@ def tile_mex_kernel(tc, x, offsets, out):
                 state["hm_ps"] = hm_ps
 
             def second():
-                hm_t = treep.tile([P, W], BF16, name="hm_t")
+                hm_t = const.tile([P, W], BF16, name="hm_t%d" % bp)
                 nc.vector.tensor_copy(out=hm_t[:], in_=state["hm_ps"][:, 0, 0:W])
+                nh = const.tile([P, W], F32, name="neg_hm%d" % bp)
+                nc.vector.tensor_scalar(out=nh[:], in0=hm_t[:], scalar1=-1.0, scalar2=None, op0=ALU.mult)
+                neg_hm[bp] = nh
                 v1 = treep.tile([P, W - 1], BF16, name="v1")
                 nc.vector.tensor_tensor(out=v1[:], in0=hm_t[:, 0:66], in1=hm_t[:, 1:67], op=ALU.max)
-                mt = const.tile([P, WO], BF16, name="m_t" + key)
+                mt = const.tile([P, WO], BF16, name="m_t%d" % bp)
                 nc.vector.tensor_tensor(out=mt[:], in0=v1[:, 0:64], in1=v1[:, 2:66], op=ALU.max)
-                m_t[key] = mt
-                rep = treep.tile([P, WO, 2], BF16, name="rep")
-                nc.vector.tensor_copy(out=rep[:], in_=mt[:].unsqueeze(2).to_broadcast([P, WO, 2]))
-                nm_ps = ps_mb.tile([P, 8, P], BF16, tag="mb", name="nm_ps")
-                nc.tensor.transpose(nm_ps[:, 0, :], rep[:].rearrange("p j u -> p (j u)"), ident[:])
-                state["nm_ps"] = nm_ps
+                m_t[bp] = mt
+                r_arg = const.tile([P, WO, 4], F32, name="r_arg%d" % bp)
+                for dh in range(4):
+                    nc.vector.tensor_tensor(
+                        out=r_arg[:, :, dh], in0=hm_t[:, dh : dh + WO], in1=mt[:], op=ALU.subtract
+                    )
+                state["r_arg"] = r_arg
 
             def third():
-                nm = const.tile([P, P], F32, name="negm" + key)
-                nc.vector.tensor_scalar(
-                    out=nm[:], in0=state["nm_ps"][:, 0, :], scalar1=-1.0, scalar2=None, op0=ALU.mult
+                rr = const.tile([P, WO, 4], F32, name="r_t%d" % bp)
+                nc.scalar.activation(
+                    out=rr[:].rearrange("p h d -> p (h d)"),
+                    in_=state["r_arg"][:].rearrange("p h d -> p (h d)"),
+                    func=ACT.Exp,
                 )
-                negm[key] = nm
+                r_t[bp] = rr
 
             return [first, second, third]
 
-        def make_m(key, blk):
+        def make_m(bp, blk):
             t = ps_mb.tile([P, 8, P], BF16, tag="mb", name="m_bc")
             for r in range(8):
                 h = 8 * blk + r
-                nc.tensor.transpose(t[:, r, :], m_t[key][:, h : h + 1].to_broadcast([P, P]), ident[:])
+                nc.tensor.transpose(t[:, r, :], m_t[bp][:, h : h + 1].to_broadcast([P, P]), ident[:])
             return t
 
-        for task in channel_max_tasks(0) + pair_tasks(0, "0a"):
+        for task in channel_max_tasks(0) + channel_max_tasks(1) + pair_tasks(0):
             task()
         nc.vector.quantize_mx(
             out=eb_codes[:].bitcast(FP8X4),
             scales=eb_scales[:],
             in_=eb_g[:].rearrange("q s m t -> q (s m t)"),
         )
-        background = channel_max_tasks(1) + pair_tasks(0, "0")
-        background = background + channel_max_tasks(2) + channel_max_tasks(3) + pair_tasks(1, "1")
-        bias_key = {0: "0a", 1: "0", 2: "1", 3: "1"}
+        background = channel_max_tasks(2) + channel_max_tasks(3) + pair_tasks(1)
 
         sums = {}
-        for b in range(4):
-            sums[b] = spool.tile([P, WO, WO], F32, name="sum%d" % b)
+        for bp in range(2):
+            sums[bp] = spool.tile([P, 2, WO, WO], F32, name="sum%d" % bp)
+        e1_t = {}
         ex_t = {}
         tp_t = {}
         g_t = {}
         q_t = {}
         acc_t = {}
 
-        def act(i, wi):
-            b = i // 16
-            w = 4 * (i % 16) + wi
-            ex = epool.tile([P, 512], BF16, name="ex")
-            xv = xh[b][:, :, 0 : 2 * W].rearrange("p c (r z) -> p c r z", r=2)
-            col = WO * (b % 2) + w
-            nc.scalar.activation(
-                out=ex[:].rearrange("p (c r d) -> p c r d", c=C, r=2, d=4),
-                in_=xv[:, :, :, w : w + 4],
-                func=ACT.Exp,
-                bias=negm[bias_key[b]][:, col : col + 1],
-                scale=1.0,
+        def rows_needed(n):
+            bp, h = divmod(min(n, UNITS - 1), WO)
+            return NI * bp + (h + 3) // 2 + 1
+
+        x1_t = {}
+
+        def t1(idx):
+            bp, i = divmod(idx, NI)
+            x1 = ps_x1.tile([P, 4, P], BF16, name="x1")
+            for dw in range(4):
+                nc.tensor.transpose(x1[:, dw, :], xc[bp][:, dw, i, :, :].rearrange("p b w -> p (b w)"), perm[:])
+            x1_t[idx] = x1
+
+        def e1_rows(idx):
+            bp, i = divmod(idx, NI)
+            for rho in range(2):
+                y = 2 * i + rho
+                if y < W:
+                    e1 = e1p.tile([P, 256], F32, name="e1")
+                    nc.scalar.activation(
+                        out=e1[:].rearrange("p (c d) -> p c d", d=4),
+                        in_=x1_t[idx][:, :, 64 * rho : 64 * rho + 64].rearrange("p d c -> p c d"),
+                        func=ACT.Exp,
+                        bias=neg_hm[bp][:, y : y + 1],
+                        scale=1.0,
+                    )
+                    e1_t[(bp, y)] = e1
+
+        def mult(n):
+            bp, h = divmod(n, WO)
+            ex = epool.tile([P, K], BF16, name="ex")
+            for dh in range(4):
+                nc.vector.tensor_scalar(
+                    out=ex[:, 256 * dh : 256 * dh + 256],
+                    in0=e1_t[(bp, h + dh)][:],
+                    scalar1=r_t[bp][:, h, dh : dh + 1],
+                    scalar2=None,
+                    op0=ALU.mult,
+                )
+            ex_t[n] = ex
+
+        def t2(n):
+            tp = ps_tp.tile([P, 4, P], F32, name="tp")
+            words = ex_t[n][:].bitcast(F32)
+            for dh in range(4):
+                nc.tensor.transpose(tp[:, dh, :], words[:, P * dh : P * dh + P], ident_f[:])
+            tp_t[n] = tp
+
+        def cpo(n):
+            gi, j4 = divmod(n, 4)
+            if j4 == 0:
+                g_t[gi] = gpool.tile([P, 2, 2048], BF16, name="g", align_bytes=64)
+            gw = g_t[gi][:].rearrange("q s k -> q (s k)").bitcast(F32).rearrange("q (s k) -> q s k", s=2)
+            nc.scalar.copy(
+                out=gw[:, :, 256 * j4 : 256 * j4 + 256].rearrange("q s (n u) -> q s n u", u=2),
+                in_=tp_t[n][:].rearrange("q (s u) n -> q s n u", s=2, u=2),
             )
-            ex_t[(i, wi)] = ex
 
-        def tr(i, wi):
-            if wi == 0:
-                for s in range(2):
-                    tp_t[(i, s)] = ps_tp.tile([P, 4, P], F32, name="tp")
-            words = ex_t[(i, wi)][:].bitcast(F32)
-            for s in range(2):
-                nc.tensor.transpose(tp_t[(i, s)][:, wi, :], words[:, P * s : P * s + P], ident_f[:])
-
-        def cp(i, s):
-            gi = i // 2
-            if i % 2 == 0:
-                g_t[(gi, s)] = gpool.tile([P, 2048], BF16, name="g", align_bytes=64)
-            lo = 512 * (i % 2)
-            nc.vector.tensor_copy(
-                out=g_t[(gi, s)][:].bitcast(F32)[:, lo : lo + 512],
-                in_=tp_t[(i, s)][:].rearrange("q w n -> q (w n)"),
+        def quant(gi):
+            codes = cpool.tile([P, 1024], U32, name="codes", align_bytes=64)
+            scales = cpool.tile([P, 1024], U8, name="scales", align_bytes=64)
+            nc.vector.quantize_mx(
+                out=codes[:].bitcast(FP8X4), scales=scales[:], in_=g_t[gi][:].rearrange("q s k -> q (s k)")
             )
-
-        def quant(gi, s):
-            codes = cpool.tile([P, 512], U32, name="codes", align_bytes=64)
-            scales = cpool.tile([P, 512], U8, name="scales", align_bytes=64)
-            nc.vector.quantize_mx(out=codes[:].bitcast(FP8X4), scales=scales[:], in_=g_t[(gi, s)][:])
-            q_t[(gi, s)] = (codes, scales)
+            q_t[gi] = (codes, scales)
 
         def mx(gi, s):
             if s == 0:
                 acc_t[gi] = ps_acc.tile([P, 512], F32, name="acc")
-            codes, scales = q_t[(gi, s)]
+            codes, scales = q_t[gi]
             nc.tensor.matmul_mx(
                 out=acc_t[gi][:],
                 lhsT=eb_codes[:, P * s : P * s + P].bitcast(FP8X4),
                 lhsT_scale=eb_scales[:, P * s : P * s + P],
-                rhs=codes[:].bitcast(FP8X4),
-                rhs_scale=scales[:],
+                rhs=codes[:, 512 * s : 512 * s + 512].bitcast(FP8X4),
+                rhs_scale=scales[:, 512 * s : 512 * s + 512],
                 start=(s == 0),
                 stop=(s == 1),
             )
 
-        def acc_copy(gi):
-            b = gi // 8
-            w0 = 8 * (gi % 8)
-            nc.vector.tensor_copy(
-                out=sums[b][:, :, w0 : w0 + 8],
-                in_=acc_t[gi][:].rearrange("m (w j) -> m j w", w=8),
-            )
+        def sum_view(gi):
+            bp, g16 = divmod(gi, 16)
+            return sums[bp][:, :, 4 * g16 : 4 * g16 + 4, :].rearrange("m b h w -> m h b w")
 
-        def log_of(b, r0, rows):
-            v = sums[b][:, r0 : r0 + rows, :].rearrange("m j w -> m (j w)")
+        def acc_view(gi):
+            return acc_t[gi][:].rearrange("m (h b w) -> m h b w", h=4, b=2)
+
+        def acc_copy(gi):
+            if gi % 2 == 1:
+                nc.vector.tensor_copy(out=sum_view(gi), in_=acc_view(gi))
+            else:
+                nc.scalar.copy(out=sum_view(gi), in_=acc_view(gi))
+
+        def log_acc(gi):
+            nc.scalar.activation(out=sum_view(gi), in_=acc_view(gi), func=ACT.Ln)
+
+        def log_of(bp, b2, r0, rows):
+            v = sums[bp][:, b2, r0 : r0 + rows, :].rearrange("m h w -> m (h w)")
             nc.scalar.activation(out=v, in_=v, func=ACT.Ln)
 
-        def finish(b, blk, m_bc):
-            v = sums[b][:, 8 * blk : 8 * blk + 8, :]
-            nc.vector.scalar_tensor_tensor(
-                out=v,
-                in0=v,
-                scalar=cb[:, 0:1],
-                in1=m_bc[:].rearrange("p h (b w) -> p h b w", b=2)[:, :, b % 2, :],
-                op0=ALU.add,
-                op1=ALU.add,
-            )
+        def finish(bp, blk):
+            m_bc = make_m(bp, blk)
+            for b2 in range(2):
+                v = sums[bp][:, b2, 8 * blk : 8 * blk + 8, :]
+                nc.vector.scalar_tensor_tensor(
+                    out=v,
+                    in0=v,
+                    scalar=cb[:, 0:1],
+                    in1=m_bc[:].rearrange("p h (b w) -> p h b w", b=2)[:, :, b2, :],
+                    op0=ALU.add,
+                    op1=ALU.add,
+                )
 
-        def store(b, r0, rows):
-            nc.sync.dma_start(
-                out=out[b, :, r0 : r0 + rows, :].rearrange("m h w -> m (h w)"),
-                in_=sums[b][:, r0 : r0 + rows, :].rearrange("m j w -> m (j w)"),
-            )
+        def store(bp, r0, rows):
+            for b2 in range(2):
+                nc.sync.dma_start(
+                    out=out[2 * bp + b2, :, r0 : r0 + rows, :].rearrange("m h w -> m (h w)"),
+                    in_=sums[bp][:, b2, r0 : r0 + rows, :].rearrange("m h w -> m (h w)"),
+                )
 
-        def phase_one():
-            for half in range(2):
-                log_of(0, 32 * half, 32)
-                log_of(1, 32 * half, 32)
-                for blk in range(4 * half, 4 * half + 4):
-                    m_bc = make_m("0", blk)
-                    finish(0, blk, m_bc)
-                    finish(1, blk, m_bc)
-                store(0, 32 * half, 32)
-                store(1, 32 * half, 32)
-            for half in range(2):
-                log_of(2, 32 * half, 32)
-                for blk in range(4 * half, 4 * half + 4):
-                    finish(2, blk, make_m("1", blk))
-                store(2, 32 * half, 32)
+        def phase(bp, blk0, blk1):
+            for blk in range(blk0, blk1):
+                for b2 in range(2):
+                    log_of(bp, b2, 8 * blk, 8)
+                finish(bp, blk)
+                if blk % 2 == 1:
+                    store(bp, 8 * (blk - 1), 16)
 
-        for i in range(QUADS + 3):
-            odd_g = (i - 3) // 2 if (i % 2 == 1 and i >= 3) else None
-            if i < QUADS:
-                for wi in range(4):
-                    act(i, wi)
-                    tr(i, wi)
-            if 1 <= i <= QUADS:
-                cp(i - 1, 0)
-            if odd_g is not None:
-                quant(odd_g, 0)
-            if 1 <= i <= QUADS:
-                cp(i - 1, 1)
-            if odd_g is not None:
-                quant(odd_g, 1)
-                mx(odd_g, 0)
-                mx(odd_g, 1)
-            if i % 2 == 0 and i >= 4:
-                acc_copy((i - 4) // 2)
-            if i >= 3 and background:
+        t1_done = 0
+        e1_done = 0
+        for n in range(UNITS + 5):
+            if n < PHASE2_AT:
+                target = rows_needed(n + 3)
+                for idx in range(t1_done, target):
+                    t1(idx)
+                t1_done = max(t1_done, target)
+            if 1 <= n <= UNITS:
+                t2(n - 1)
+            if n % 4 == 3 and n >= 7:
+                mx((n - 7) // 4, 0)
+                mx((n - 7) // 4, 1)
+            if n < PHASE2_AT:
+                target = rows_needed(n + 2)
+                for idx in range(e1_done, target):
+                    e1_rows(idx)
+                e1_done = max(e1_done, target)
+            if n == PHASE2_AT:
+                for idx in range(e1_done, 2 * NI):
+                    if idx >= t1_done:
+                        t1(idx)
+                    e1_rows(idx)
+            if 2 <= n <= UNITS + 1:
+                cpo(n - 2)
+            if n % 4 == 0 and n >= 8:
+                gi = (n - 8) // 4
+                if n <= PHASE2_AT:
+                    acc_copy(gi)
+                else:
+                    log_acc(gi)
+                    if gi % 2 == 1:
+                        blk = (gi % 16) // 2
+                        finish(1, blk)
+                        store(1, 8 * blk, 8)
+            if n < UNITS:
+                mult(n)
+            if n % 4 == 2 and n >= 6:
+                quant((n - 6) // 4)
+            if n >= BG_START and background:
                 task = background[0]
                 task()
                 background = background[1:]
-            if i == PHASE_AT:
-                phase_one()
-
-        for qd in range(4):
-            log_of(3, 16 * qd, 16)
-            for blk in (2 * qd, 2 * qd + 1):
-                finish(3, blk, make_m("1", blk))
-            store(3, 16 * qd, 16)
+            if n == PHASE1_AT:
+                phase(0, 0, 8)
+            if n == PHASE2_AT:
+                phase(1, 0, 6)

@@ -313,8 +313,8 @@ def tile_mex_kernel(tc, x, offsets, out):
             )
             q_t[gi] = (codes, scales)
 
-        def mx(gi, s):
-            if s == 0:
+        def mx(gi, s, first):
+            if s == 0 and first:
                 acc_t[gi] = ps_acc.tile([P, 512], F32, name="acc")
             codes, scales = q_t[gi]
             nc.tensor.matmul_mx(
@@ -386,8 +386,9 @@ def tile_mex_kernel(tc, x, offsets, out):
             if 1 <= n <= UNITS:
                 t2(n - 1)
             if n % 4 == 3 and n >= 7:
-                mx((n - 7) // 4, 0)
-                mx((n - 7) // 4, 1)
+                for rep in range(2):
+                    mx((n - 7) // 4, 0, rep == 0)
+                    mx((n - 7) // 4, 1, rep == 0)
             if n < PHASE2_AT:
                 target = rows_needed(n + 2)
                 for idx in range(e1_done, target):

@@ -23,11 +23,12 @@ WO = 64
 K = 1024
 NI = 34
 UNITS = 128
+LEAD = 6
 PHASE1_AT = 68
 PHASE2_AT = 116
 BG_START = 30
-CHUNKS0 = ((0, 4), (4, 9), (9, 16))
-CHUNKS0B = ((16, 25), (25, 34))
+CHUNKS0 = ((0, 4), (4, 9), (9, 16), (16, 25))
+CHUNKS0B = ((25, 34),)
 CHUNKS1 = ((0, 8), (8, 20), (20, 34))
 
 
@@ -39,14 +40,14 @@ def tile_mex_kernel(tc, x, offsets, out):
         xcp = ctx.enter_context(tc.tile_pool(name="xc", bufs=1))
         cmxp = ctx.enter_context(tc.tile_pool(name="cmx", bufs=2))
         treep = ctx.enter_context(tc.tile_pool(name="tree", bufs=1))
-        e1p = ctx.enter_context(tc.tile_pool(name="e1", bufs=18))
-        epool = ctx.enter_context(tc.tile_pool(name="ex", bufs=4))
+        e1p = ctx.enter_context(tc.tile_pool(name="e1", bufs=16))
+        epool = ctx.enter_context(tc.tile_pool(name="ex", bufs=6))
         gpool = ctx.enter_context(tc.tile_pool(name="grouped", bufs=2))
         cpool = ctx.enter_context(tc.tile_pool(name="codes", bufs=2))
         spool = ctx.enter_context(tc.tile_pool(name="sums", bufs=1))
         ps_x1 = ctx.enter_context(tc.psum_pool(name="ps_x1", bufs=2))
-        ps_tp = ctx.enter_context(tc.psum_pool(name="ps_tp", bufs=2))
-        ps_acc = ctx.enter_context(tc.psum_pool(name="ps_acc", bufs=2))
+        ps_tp = ctx.enter_context(tc.psum_pool(name="ps_tp", bufs=3))
+        ps_acc = ctx.enter_context(tc.psum_pool(name="ps_acc", bufs=1))
         ps_mb = ctx.enter_context(tc.psum_pool(name="ps_mb", bufs=2))
 
         ident = const.tile([P, P], BF16, name="ident")
@@ -313,8 +314,8 @@ def tile_mex_kernel(tc, x, offsets, out):
             )
             q_t[gi] = (codes, scales)
 
-        def mx(gi, s, first):
-            if s == 0 and first:
+        def mx(gi, s):
+            if s == 0:
                 acc_t[gi] = ps_acc.tile([P, 512], F32, name="acc")
             codes, scales = q_t[gi]
             nc.tensor.matmul_mx(
@@ -377,20 +378,13 @@ def tile_mex_kernel(tc, x, offsets, out):
 
         t1_done = 0
         e1_done = 0
-        for n in range(UNITS + 5):
+        for n in range(-LEAD, UNITS + 5):
             if n < PHASE2_AT:
-                target = rows_needed(n + 3)
+                target = rows_needed(max(n + LEAD + 2, 0))
                 for idx in range(t1_done, target):
                     t1(idx)
                 t1_done = max(t1_done, target)
-            if 1 <= n <= UNITS:
-                t2(n - 1)
-            if n % 4 == 3 and n >= 7:
-                for rep in range(2):
-                    mx((n - 7) // 4, 0, rep == 0)
-                    mx((n - 7) // 4, 1, rep == 0)
-            if n < PHASE2_AT:
-                target = rows_needed(n + 2)
+                target = rows_needed(max(n + LEAD + 1, 0))
                 for idx in range(e1_done, target):
                     e1_rows(idx)
                 e1_done = max(e1_done, target)
@@ -399,8 +393,16 @@ def tile_mex_kernel(tc, x, offsets, out):
                     if idx >= t1_done:
                         t1(idx)
                     e1_rows(idx)
-            if 2 <= n <= UNITS + 1:
-                cpo(n - 2)
+            if 0 <= n < UNITS:
+                t2(n)
+                cpo(n)
+            if n % 4 == 3 and 3 <= n < UNITS:
+                quant(n // 4)
+            if 0 <= n + LEAD < UNITS:
+                mult(n + LEAD)
+            if n % 4 == 3 and n >= 7 and (n - 7) // 4 < 32:
+                mx((n - 7) // 4, 0)
+                mx((n - 7) // 4, 1)
             if n % 4 == 0 and n >= 8:
                 gi = (n - 8) // 4
                 if n <= PHASE2_AT:
@@ -411,10 +413,6 @@ def tile_mex_kernel(tc, x, offsets, out):
                         blk = (gi % 16) // 2
                         finish(1, blk)
                         store(1, 8 * blk, 8)
-            if n < UNITS:
-                mult(n)
-            if n % 4 == 2 and n >= 6:
-                quant((n - 6) // 4)
             if n >= BG_START and background:
                 task = background[0]
                 task()

@@ -376,6 +376,24 @@ def tile_mex_kernel(tc, x, offsets, out):
                 if blk % 2 == 1:
                     store(bp, 8 * (blk - 1), 16)
 
+        warm = {}
+
+        def new_warm():
+            warm["t"] = ps_mb.tile([P, 512], F32, tag="mb", name="warm")
+
+        def keep_clock():
+            for rep in range(4):
+                nc.tensor.matmul_mx(
+                    out=warm["t"][:, 0:256],
+                    lhsT=eb_codes[:, 0:P].bitcast(FP8X4),
+                    lhsT_scale=eb_scales[:, 0:P],
+                    rhs=eb_codes[:, 0:256].bitcast(FP8X4),
+                    rhs_scale=eb_scales[:, 0:256],
+                    start=True,
+                    stop=True,
+                )
+
+        new_warm()
         t1_done = 0
         e1_done = 0
         for n in range(-LEAD, UNITS + 5):
@@ -400,6 +418,8 @@ def tile_mex_kernel(tc, x, offsets, out):
                 quant(n // 4)
             if 0 <= n + LEAD < UNITS:
                 mult(n + LEAD)
+            if (n < 0 or n % 4 == 1) and n < UNITS:
+                keep_clock()
             if n % 4 == 3 and n >= 7 and (n - 7) // 4 < 32:
                 mx((n - 7) // 4, 0)
                 mx((n - 7) // 4, 1)
@@ -419,5 +439,7 @@ def tile_mex_kernel(tc, x, offsets, out):
                 background = background[1:]
             if n == PHASE1_AT:
                 phase(0, 0, 8)
+                new_warm()
             if n == PHASE2_AT:
                 phase(1, 0, 6)
+                new_warm()

@@ -280,13 +280,21 @@ def tile_mex_kernel(tc, x, offsets, out):
             bp, h = divmod(n, WO)
             ex = epool.tile([P, K], BF16, name="ex")
             for dh in range(4):
-                nc.vector.tensor_scalar(
-                    out=ex[:, 256 * dh : 256 * dh + 256],
-                    in0=e1_t[(bp, h + dh)][:],
-                    scalar1=r_t[bp][:, h, dh : dh + 1],
-                    scalar2=None,
-                    op0=ALU.mult,
-                )
+                if dh == 3 and n % 2 == 1:
+                    nc.scalar.activation(
+                        out=ex[:, 256 * dh : 256 * dh + 256],
+                        in_=e1_t[(bp, h + dh)][:],
+                        func=ACT.Copy,
+                        scale=r_t[bp][:, h, dh : dh + 1],
+                    )
+                else:
+                    nc.vector.tensor_scalar(
+                        out=ex[:, 256 * dh : 256 * dh + 256],
+                        in0=e1_t[(bp, h + dh)][:],
+                        scalar1=r_t[bp][:, h, dh : dh + 1],
+                        scalar2=None,
+                        op0=ALU.mult,
+                    )
             ex_t[n] = ex
 
         def t2(n):
@@ -336,10 +344,7 @@ def tile_mex_kernel(tc, x, offsets, out):
             return acc_t[gi][:].rearrange("m (h b w) -> m h b w", h=4, b=2)
 
         def acc_copy(gi):
-            if gi % 2 == 1:
-                nc.vector.tensor_copy(out=sum_view(gi), in_=acc_view(gi))
-            else:
-                nc.scalar.copy(out=sum_view(gi), in_=acc_view(gi))
+            nc.scalar.copy(out=sum_view(gi), in_=acc_view(gi))
 
         def log_acc(gi):
             nc.scalar.activation(out=sum_view(gi), in_=acc_view(gi), func=ACT.Ln)
@@ -376,24 +381,6 @@ def tile_mex_kernel(tc, x, offsets, out):
                 if blk % 2 == 1:
                     store(bp, 8 * (blk - 1), 16)
 
-        warm = {}
-
-        def new_warm():
-            warm["t"] = ps_mb.tile([P, 512], F32, tag="mb", name="warm")
-
-        def keep_clock():
-            for rep in range(4):
-                nc.tensor.matmul_mx(
-                    out=warm["t"][:, 0:256],
-                    lhsT=eb_codes[:, 0:P].bitcast(FP8X4),
-                    lhsT_scale=eb_scales[:, 0:P],
-                    rhs=eb_codes[:, 0:256].bitcast(FP8X4),
-                    rhs_scale=eb_scales[:, 0:256],
-                    start=True,
-                    stop=True,
-                )
-
-        new_warm()
         t1_done = 0
         e1_done = 0
         for n in range(-LEAD, UNITS + 5):
@@ -418,8 +405,6 @@ def tile_mex_kernel(tc, x, offsets, out):
                 quant(n // 4)
             if 0 <= n + LEAD < UNITS:
                 mult(n + LEAD)
-            if (n < 0 or n % 4 == 1) and n < UNITS:
-                keep_clock()
             if n % 4 == 3 and n >= 7 and (n - 7) // 4 < 32:
                 mx((n - 7) // 4, 0)
                 mx((n - 7) // 4, 1)
@@ -439,7 +424,5 @@ def tile_mex_kernel(tc, x, offsets, out):
                 background = background[1:]
             if n == PHASE1_AT:
                 phase(0, 0, 8)
-                new_warm()
             if n == PHASE2_AT:
                 phase(1, 0, 6)
-                new_warm()

@@ -280,7 +280,7 @@ def tile_mex_kernel(tc, x, offsets, out):
             bp, h = divmod(n, WO)
             ex = epool.tile([P, K], BF16, name="ex")
             for dh in range(4):
-                if dh == 3 and n % 2 == 1:
+                if dh == 3 and n % 8 == 3:
                     nc.scalar.activation(
                         out=ex[:, 256 * dh : 256 * dh + 256],
                         in_=e1_t[(bp, h + dh)][:],

@@ -21,15 +21,14 @@ C = 64
 W = 67
 WO = 64
 K = 1024
-NI = 34
+HH = 32
+YH = HH + 3
 UNITS = 128
 LEAD = 6
 PHASE1_AT = 68
 PHASE2_AT = 116
-BG_START = 30
-CHUNKS0 = ((0, 4), (4, 9), (9, 16), (16, 25))
-CHUNKS0B = ((25, 34),)
-CHUNKS1 = ((0, 8), (8, 20), (20, 34))
+PREPARE_AT = {(0, 1): -4, (0, 2): 14, (1, 0): 26, (1, 1): 44, (1, 2): 70}
+CHUNKS = ((0, 12), (12, 24), (24, YH))
 
 
 def tile_mex_kernel(tc, x, offsets, out):
@@ -37,10 +36,9 @@ def tile_mex_kernel(tc, x, offsets, out):
     with ExitStack() as ctx:
         ctx.enter_context(tc.manual_schedule())
         const = ctx.enter_context(tc.tile_pool(name="const", bufs=1))
-        xcp = ctx.enter_context(tc.tile_pool(name="xc", bufs=1))
-        cmxp = ctx.enter_context(tc.tile_pool(name="cmx", bufs=2))
-        treep = ctx.enter_context(tc.tile_pool(name="tree", bufs=1))
-        e1p = ctx.enter_context(tc.tile_pool(name="e1", bufs=16))
+        rawp = ctx.enter_context(tc.tile_pool(name="raw", bufs=1))
+        winp = ctx.enter_context(tc.tile_pool(name="win", bufs=2))
+        e1p = ctx.enter_context(tc.tile_pool(name="e1", bufs=32))
         epool = ctx.enter_context(tc.tile_pool(name="ex", bufs=6))
         gpool = ctx.enter_context(tc.tile_pool(name="grouped", bufs=2))
         cpool = ctx.enter_context(tc.tile_pool(name="codes", bufs=2))
@@ -60,187 +58,164 @@ def tile_mex_kernel(tc, x, offsets, out):
             in_=ident[:].rearrange("p (x i g e) -> p x g i e", x=4, i=4, g=4, e=2),
         )
 
+        raw = {}
+
+        def load_chunk(bp, ci):
+            y0, y1 = CHUNKS[ci]
+            raw[(bp, ci)] = rawp.tile([P, 2, 816], BF16, name="raw%d_%d" % (bp, ci))
+            for q in range(2):
+                nc.sync.dma_start(
+                    out=raw[(bp, ci)][:, q, 0 : W * (y1 - y0)],
+                    in_=x[2 * bp : 2 * bp + 2, :, HH * q + y0 : HH * q + y1, :].rearrange("b c y z -> (b c) (y z)"),
+                )
+
+        load_chunk(0, 0)
         offs = const.tile([P, K], BF16, name="offs")
         nc.sync.dma_start(out=offs[:], in_=offsets[0].rearrange("m c i j -> m (c i j)"))
-
-        cmx = {}
-        xc = {}
-        for bp in range(2):
-            xc[bp] = xcp.tile([P, 4, NI, 2, WO], BF16, name="xc%d" % bp)
-            nc.vector.memset(xc[bp][64:128, :, NI - 1, :, :], 0.0)
-
-        def load_cmx(b):
-            t = cmxp.tile([P, C * W], BF16, name="cmx")
-            v = t[:].rearrange("y (c z) -> y c z", z=W)
-            nc.sync.dma_start(out=v[0:64], in_=x[b, :, 0:64, :].rearrange("c y z -> y c z"))
-            nc.sync.dma_start(out=v[64:67], in_=x[b, :, 64:67, :].rearrange("c y z -> y c z"))
-            cmx[b] = t
-
-        def load_xc(bp, i0, i1):
-            for dw in range(4):
-                for b2 in range(2):
-                    for rho in range(2):
-                        hi = min(i1, NI - rho)
-                        n = hi - i0
-                        if n > 0:
-                            y0 = 2 * i0 + rho
-                            nc.sync.dma_start(
-                                out=xc[bp][64 * rho : 64 * rho + 64, dw, i0:hi, b2, :],
-                                in_=x[2 * bp + b2, :, y0 : y0 + 2 * n - 1 : 2, dw : dw + WO],
-                            )
-
-        load_cmx(0)
-        load_cmx(1)
-        for i0, i1 in CHUNKS0:
-            load_xc(0, i0, i1)
-        load_cmx(2)
-        load_cmx(3)
-        for i0, i1 in CHUNKS0B:
-            load_xc(0, i0, i1)
-        for i0, i1 in CHUNKS1:
-            load_xc(1, i0, i1)
+        for bp, ci in ((0, 1), (0, 2), (1, 0), (1, 1), (1, 2)):
+            load_chunk(bp, ci)
 
         mb = const.tile([P, 1], F32, name="mb")
-        nc.vector.tensor_reduce(out=mb[:], in_=offs[:], axis=mybir.AxisListType.X, op=ALU.max)
         neg_mb = const.tile([P, 1], F32, name="neg_mb")
-        nc.vector.tensor_scalar(out=neg_mb[:], in0=mb[:], scalar1=-1.0, scalar2=None, op0=ALU.mult)
         cb = const.tile([P, 1], F32, name="cb")
-        nc.vector.tensor_scalar(out=cb[:], in0=mb[:], scalar1=-math.log(float(K)), scalar2=None, op0=ALU.add)
         eb_n = const.tile([P, C, 4, 4], BF16, name="eb_n")
-        nc.scalar.activation(
-            out=eb_n[:].rearrange("m c d w -> m (c d w)"), in_=offs[:], func=ACT.Exp, bias=neg_mb[:, 0:1], scale=1.0
-        )
         eb_t = const.tile([P, 4, C, 4], BF16, name="eb_t")
-        for dh in range(4):
-            for a in range(2):
-                nc.vector.tensor_copy(
-                    out=eb_t[:, dh, 32 * a : 32 * a + 32, :].rearrange("m (g i e) w -> m g i e w", g=4, i=4, e=2),
-                    in_=eb_n[:, 32 * a : 32 * a + 32, dh, :].rearrange("m (i g e) w -> m g i e w", i=4, g=4, e=2),
-                )
-        eb_w = eb_t[:].rearrange("m d c w -> m (d c w)").bitcast(F32)
-        eb_ps = ps_mb.tile([P, 4, P], F32, tag="mb", name="eb_ps")
-        for dh in range(4):
-            nc.tensor.transpose(eb_ps[:, dh, :], eb_w[:, P * dh : P * dh + P], ident_f[:])
         eb_g = const.tile([P, 2, P, 4], BF16, name="eb_g", align_bytes=64)
-        nc.vector.tensor_copy(
-            out=eb_g[:].rearrange("q s m t -> q (s m t)").bitcast(F32).rearrange("q (s m u) -> q s m u", s=2, m=P, u=2),
-            in_=eb_ps[:].rearrange("q (s u) m -> q s m u", s=2, u=2),
-        )
         eb_codes = const.tile([P, 2 * P], U32, name="eb_codes", align_bytes=64)
         eb_scales = const.tile([P, 2 * P], U8, name="eb_scales", align_bytes=64)
 
-        R = W
-        m_t = {}
-        neg_hm = {}
-        r_t = {}
-        cm = {}
-        hm_y = const.tile([P, P], BF16, name="hm_y")
-        nc.vector.memset(hm_y[:], 0.0)
-        for bp in range(2):
-            cm[bp] = const.tile([P, 2, W], BF16, name="cm%d" % bp)
+        def eb_tasks():
+            nc.vector.tensor_reduce(out=mb[:], in_=offs[:], axis=mybir.AxisListType.X, op=ALU.max)
+            nc.vector.tensor_scalar(out=neg_mb[:], in0=mb[:], scalar1=-1.0, scalar2=None, op0=ALU.mult)
+            nc.vector.tensor_scalar(out=cb[:], in0=mb[:], scalar1=-math.log(float(K)), scalar2=None, op0=ALU.add)
+            nc.scalar.activation(
+                out=eb_n[:].rearrange("m c d w -> m (c d w)"), in_=offs[:], func=ACT.Exp, bias=neg_mb[:, 0:1], scale=1.0
+            )
+            for dh in range(4):
+                for a in range(2):
+                    nc.vector.tensor_copy(
+                        out=eb_t[:, dh, 32 * a : 32 * a + 32, :].rearrange("m (g i e) w -> m g i e w", g=4, i=4, e=2),
+                        in_=eb_n[:, 32 * a : 32 * a + 32, dh, :].rearrange("m (i g e) w -> m g i e w", i=4, g=4, e=2),
+                    )
+            eb_w = eb_t[:].rearrange("m d c w -> m (d c w)").bitcast(F32)
+            eb_ps = ps_mb.tile([P, 4, P], F32, tag="mb", name="eb_ps")
+            for dh in range(4):
+                nc.tensor.transpose(eb_ps[:, dh, :], eb_w[:, P * dh : P * dh + P], ident_f[:])
+            nc.vector.tensor_copy(
+                out=eb_g[:].rearrange("q s m t -> q (s m t)").bitcast(F32).rearrange("q (s m u) -> q s m u", s=2, m=P, u=2),
+                in_=eb_ps[:].rearrange("q (s u) m -> q s m u", s=2, u=2),
+            )
 
-        def channel_max_tasks(b):
+        xi = {}
+        hm = {}
+        neg_hm = {}
+        m_t = {}
+        r_arg = {}
+        r_t = {}
+        for bp in range(2):
+            xi[bp] = rawp.tile([P, YH * W * 2], BF16, name="xi%d" % bp)
+            hm[bp] = const.tile([P, 2, YH], BF16, name="hm%d" % bp)
+            neg_hm[bp] = const.tile([P, 2, YH], F32, name="neg_hm%d" % bp)
+            m_t[bp] = const.tile([P, 2, HH], BF16, name="m_t%d" % bp)
+            r_arg[bp] = const.tile([P, 2, HH, 4], F32, name="r_arg%d" % bp)
+            r_t[bp] = const.tile([P, 2, HH, 4], F32, name="r_t%d" % bp)
+
+        def prepare_tasks(bp, ci):
+            y0, y1 = CHUNKS[ci]
+            rows = y1 - y0
+            h0, h1 = max(y0 - 3, 0), y1 - 3
             state = {}
 
-            def level0(part):
+            def interleave():
+                nc.vector.tensor_copy(
+                    out=xi[bp][:, 134 * y0 : 134 * y1].rearrange("p (f q) -> p f q", q=2),
+                    in_=raw[(bp, ci)][:, :, 0 : W * rows].rearrange("p q f -> p f q"),
+                )
+
+            def window1():
+                a1 = winp.tile([P, 134 * 12], BF16, name="a1")
+                n = 134 * rows - 2
+                nc.vector.tensor_tensor(
+                    out=a1[:, 0:n],
+                    in0=xi[bp][:, 134 * y0 : 134 * y0 + n],
+                    in1=xi[bp][:, 134 * y0 + 2 : 134 * y0 + 2 + n],
+                    op=ALU.max,
+                )
+                state["a1"] = a1
+
+            def window2():
+                a2 = winp.tile([P, 12, P], BF16, name="a2")
+                v = state["a1"][:, 0 : 134 * rows].rearrange("p (y f) -> p y f", y=rows)
+                nc.vector.tensor_tensor(
+                    out=a2[:, 0:rows, :], in0=v[:, :, 0:128], in1=v[:, :, 4:132], op=ALU.max
+                )
+                state["a2"] = a2
+
+            def channel_max(part):
                 def run():
-                    if part == 0:
-                        state["t0"] = treep.tile([P, 2144], BF16, name="tr0")
-                    lo = 1072 * part
-                    nc.vector.tensor_tensor(
-                        out=state["t0"][:R, lo : lo + 1072],
-                        in0=cmx[b][:R, lo : lo + 1072],
-                        in1=cmx[b][:R, 2144 + lo : 2144 + lo + 1072],
+                    r0, r1 = (0, min(rows, 8)) if part == 0 else (8, rows)
+                    t = ps_mb.tile([P, 8, P], BF16, tag="mb", name="hm_ps")
+                    for r in range(r0, r1):
+                        nc.tensor.transpose(t[:, r - r0, :], state["a2"][:, r, :], ident[:])
+                    nc.vector.tensor_reduce(
+                        out=hm[bp][:, :, y0 + r0 : y0 + r1].rearrange("p b y -> p y b"),
+                        in_=t[:, 0 : r1 - r0, :].rearrange("p y (b c) -> p y b c", b=2),
+                        axis=mybir.AxisListType.X,
                         op=ALU.max,
                     )
 
                 return run
 
-            def level1():
-                t1 = treep.tile([P, 1072], BF16, name="tr1")
-                nc.vector.tensor_tensor(
-                    out=t1[:R, :], in0=state["t0"][:R, 0:1072], in1=state["t0"][:R, 1072:2144], op=ALU.max
+            def position_max():
+                nc.vector.tensor_scalar(
+                    out=neg_hm[bp][:, :, y0:y1], in0=hm[bp][:, :, y0:y1], scalar1=-1.0, scalar2=None, op0=ALU.mult
                 )
-                state["t1"] = t1
-
-            def rest():
-                cur = state["t1"]
-                for lvl, half in enumerate((536, 268, 134)):
-                    nxt = treep.tile([P, half], BF16, name="tr%d" % (lvl + 2))
-                    nc.vector.tensor_tensor(
-                        out=nxt[:R, :], in0=cur[:R, 0:half], in1=cur[:R, half : 2 * half], op=ALU.max
-                    )
-                    cur = nxt
+                v1 = winp.tile([P, 2, 16], BF16, name="v1")
+                n = h1 - h0
                 nc.vector.tensor_tensor(
-                    out=cm[b // 2][:R, b % 2, :], in0=cur[:R, 0:W], in1=cur[:R, W : 2 * W], op=ALU.max
+                    out=v1[:, :, 0 : n + 2], in0=hm[bp][:, :, h0 : h1 + 2], in1=hm[bp][:, :, h0 + 1 : h1 + 3], op=ALU.max
                 )
-
-            return [level0(0), level0(1), level1, rest]
-
-        def pair_tasks(bp):
-            state = {}
-
-            def first():
-                a1 = treep.tile([P, 2, W - 1], BF16, name="a1")
-                nc.vector.tensor_tensor(out=a1[:R], in0=cm[bp][:R, :, 0:66], in1=cm[bp][:R, :, 1:67], op=ALU.max)
                 nc.vector.tensor_tensor(
-                    out=hm_y[:R].rearrange("y (b w) -> y b w", b=2),
-                    in0=a1[:R, :, 0:64],
-                    in1=a1[:R, :, 2:66],
-                    op=ALU.max,
+                    out=m_t[bp][:, :, h0:h1], in0=v1[:, :, 0:n], in1=v1[:, :, 2 : n + 2], op=ALU.max
                 )
-                hm_ps = ps_mb.tile([P, 8, P], BF16, tag="mb", name="hm_ps")
-                nc.tensor.transpose(hm_ps[:, 0, :], hm_y[:], ident[:])
-                state["hm_ps"] = hm_ps
-
-            def second():
-                hm_t = const.tile([P, W], BF16, name="hm_t%d" % bp)
-                nc.vector.tensor_copy(out=hm_t[:], in_=state["hm_ps"][:, 0, 0:W])
-                nh = const.tile([P, W], F32, name="neg_hm%d" % bp)
-                nc.vector.tensor_scalar(out=nh[:], in0=hm_t[:], scalar1=-1.0, scalar2=None, op0=ALU.mult)
-                neg_hm[bp] = nh
-                v1 = treep.tile([P, W - 1], BF16, name="v1")
-                nc.vector.tensor_tensor(out=v1[:], in0=hm_t[:, 0:66], in1=hm_t[:, 1:67], op=ALU.max)
-                mt = const.tile([P, WO], BF16, name="m_t%d" % bp)
-                nc.vector.tensor_tensor(out=mt[:], in0=v1[:, 0:64], in1=v1[:, 2:66], op=ALU.max)
-                m_t[bp] = mt
-                r_arg = const.tile([P, WO, 4], F32, name="r_arg%d" % bp)
                 for dh in range(4):
                     nc.vector.tensor_tensor(
-                        out=r_arg[:, :, dh], in0=hm_t[:, dh : dh + WO], in1=mt[:], op=ALU.subtract
+                        out=r_arg[bp][:, :, h0:h1, dh],
+                        in0=hm[bp][:, :, h0 + dh : h1 + dh],
+                        in1=m_t[bp][:, :, h0:h1],
+                        op=ALU.subtract,
                     )
-                state["r_arg"] = r_arg
 
-            def third():
-                rr = const.tile([P, WO, 4], F32, name="r_t%d" % bp)
+            def ratios():
                 nc.scalar.activation(
-                    out=rr[:].rearrange("p h d -> p (h d)"),
-                    in_=state["r_arg"][:].rearrange("p h d -> p (h d)"),
+                    out=r_t[bp][:, :, h0:h1, :].rearrange("p b h d -> p b (h d)"),
+                    in_=r_arg[bp][:, :, h0:h1, :].rearrange("p b h d -> p b (h d)"),
                     func=ACT.Exp,
                 )
-                r_t[bp] = rr
 
-            return [first, second, third]
+            return [interleave, window1, window2, channel_max(0), channel_max(1), position_max, ratios]
 
-        def make_m(bp, blk):
+        def make_m(bp, hb):
             t = ps_mb.tile([P, 8, P], BF16, tag="mb", name="m_bc")
             for r in range(8):
-                h = 8 * blk + r
-                nc.tensor.transpose(t[:, r, :], m_t[bp][:, h : h + 1].to_broadcast([P, P]), ident[:])
+                h = 4 * hb + r % 4
+                nc.tensor.transpose(t[:, r, :], m_t[bp][:, r // 4, h : h + 1].to_broadcast([P, P]), ident[:])
             return t
 
-        for task in channel_max_tasks(0) + channel_max_tasks(1) + pair_tasks(0):
+        for task in prepare_tasks(0, 0):
             task()
+        eb_tasks()
         nc.vector.quantize_mx(
             out=eb_codes[:].bitcast(FP8X4),
             scales=eb_scales[:],
             in_=eb_g[:].rearrange("q s m t -> q (s m t)"),
         )
-        background = channel_max_tasks(2) + channel_max_tasks(3) + pair_tasks(1)
+
+        background = []
 
         sums = {}
         for bp in range(2):
-            sums[bp] = spool.tile([P, 2, WO, WO], F32, name="sum%d" % bp)
+            sums[bp] = spool.tile([P, 2, 2, HH, WO], F32, name="sum%d" % bp)
         e1_t = {}
         ex_t = {}
         tp_t = {}
@@ -248,50 +223,55 @@ def tile_mex_kernel(tc, x, offsets, out):
         q_t = {}
         acc_t = {}
 
+        def unit(n):
+            bp, r = divmod(n, 64)
+            hb, r = divmod(r, 8)
+            b2, j = divmod(r, 4)
+            return bp, b2, 4 * hb + j
+
         def rows_needed(n):
-            bp, h = divmod(min(n, UNITS - 1), WO)
-            return NI * bp + (h + 3) // 2 + 1
+            bp, b2, h = unit(min(n, UNITS - 1))
+            return YH * bp + h + 4
 
         x1_t = {}
 
         def t1(idx):
-            bp, i = divmod(idx, NI)
+            bp, y = divmod(idx, YH)
             x1 = ps_x1.tile([P, 4, P], BF16, name="x1")
             for dw in range(4):
-                nc.tensor.transpose(x1[:, dw, :], xc[bp][:, dw, i, :, :].rearrange("p b w -> p (b w)"), perm[:])
+                f = 134 * y + 2 * dw
+                nc.tensor.transpose(x1[:, dw, :], xi[bp][:, f : f + P], perm[:])
             x1_t[idx] = x1
 
         def e1_rows(idx):
-            bp, i = divmod(idx, NI)
-            for rho in range(2):
-                y = 2 * i + rho
-                if y < W:
-                    e1 = e1p.tile([P, 256], F32, name="e1")
-                    nc.scalar.activation(
-                        out=e1[:].rearrange("p (c d) -> p c d", d=4),
-                        in_=x1_t[idx][:, :, 64 * rho : 64 * rho + 64].rearrange("p d c -> p c d"),
-                        func=ACT.Exp,
-                        bias=neg_hm[bp][:, y : y + 1],
-                        scale=1.0,
-                    )
-                    e1_t[(bp, y)] = e1
+            bp, y = divmod(idx, YH)
+            for b2 in range(2):
+                e1 = e1p.tile([P, 256], F32, name="e1")
+                nc.scalar.activation(
+                    out=e1[:].rearrange("p (c d) -> p c d", d=4),
+                    in_=x1_t[idx][:, :, 64 * b2 : 64 * b2 + 64].rearrange("p d c -> p c d"),
+                    func=ACT.Exp,
+                    bias=neg_hm[bp][:, b2, y : y + 1],
+                    scale=1.0,
+                )
+                e1_t[(bp, b2, y)] = e1
 
         def mult(n):
-            bp, h = divmod(n, WO)
+            bp, b2, h = unit(n)
             ex = epool.tile([P, K], BF16, name="ex")
             for dh in range(4):
                 if dh == 3 and n % 8 == 3:
                     nc.scalar.activation(
                         out=ex[:, 256 * dh : 256 * dh + 256],
-                        in_=e1_t[(bp, h + dh)][:],
+                        in_=e1_t[(bp, b2, h + dh)][:],
                         func=ACT.Copy,
-                        scale=r_t[bp][:, h, dh : dh + 1],
+                        scale=r_t[bp][:, b2, h, dh : dh + 1],
                     )
                 else:
                     nc.vector.tensor_scalar(
                         out=ex[:, 256 * dh : 256 * dh + 256],
-                        in0=e1_t[(bp, h + dh)][:],
-                        scalar1=r_t[bp][:, h, dh : dh + 1],
+                        in0=e1_t[(bp, b2, h + dh)][:],
+                        scalar1=r_t[bp][:, b2, h, dh : dh + 1],
                         scalar2=None,
                         op0=ALU.mult,
                     )
@@ -338,10 +318,11 @@ def tile_mex_kernel(tc, x, offsets, out):
 
         def sum_view(gi):
             bp, g16 = divmod(gi, 16)
-            return sums[bp][:, :, 4 * g16 : 4 * g16 + 4, :].rearrange("m b h w -> m h b w")
+            hb, b2 = divmod(g16, 2)
+            return sums[bp][:, b2, :, 4 * hb : 4 * hb + 4, :].rearrange("m q h w -> m q (h w)")
 
         def acc_view(gi):
-            return acc_t[gi][:].rearrange("m (h b w) -> m h b w", h=4, b=2)
+            return acc_t[gi][:].rearrange("m (f q) -> m q f", q=2)
 
         def acc_copy(gi):
             nc.scalar.copy(out=sum_view(gi), in_=acc_view(gi))
@@ -349,55 +330,46 @@ def tile_mex_kernel(tc, x, offsets, out):
         def log_acc(gi):
             nc.scalar.activation(out=sum_view(gi), in_=acc_view(gi), func=ACT.Ln)
 
-        def log_of(bp, b2, r0, rows):
-            v = sums[bp][:, b2, r0 : r0 + rows, :].rearrange("m h w -> m (h w)")
-            nc.scalar.activation(out=v, in_=v, func=ACT.Ln)
-
-        def finish(bp, blk):
-            m_bc = make_m(bp, blk)
+        def finish(bp, hb):
+            m_bc = make_m(bp, hb)
             for b2 in range(2):
-                v = sums[bp][:, b2, 8 * blk : 8 * blk + 8, :]
+                v = sum_view(16 * bp + 2 * hb + b2)
                 nc.vector.scalar_tensor_tensor(
                     out=v,
                     in0=v,
                     scalar=cb[:, 0:1],
-                    in1=m_bc[:].rearrange("p h (b w) -> p h b w", b=2)[:, :, b2, :],
+                    in1=m_bc[:, 4 * b2 : 4 * b2 + 4, :].rearrange("p h (w q) -> p q (h w)", q=2),
                     op0=ALU.add,
                     op1=ALU.add,
                 )
 
         def store(bp, r0, rows):
             for b2 in range(2):
-                nc.sync.dma_start(
-                    out=out[2 * bp + b2, :, r0 : r0 + rows, :].rearrange("m h w -> m (h w)"),
-                    in_=sums[bp][:, b2, r0 : r0 + rows, :].rearrange("m h w -> m (h w)"),
-                )
+                for q in range(2):
+                    nc.sync.dma_start(
+                        out=out[2 * bp + b2, :, HH * q + r0 : HH * q + r0 + rows, :].rearrange("m h w -> m (h w)"),
+                        in_=sums[bp][:, b2, q, r0 : r0 + rows, :].rearrange("m h w -> m (h w)"),
+                    )
 
-        def phase(bp, blk0, blk1):
-            for blk in range(blk0, blk1):
+        def phase(bp, hb0, hb1):
+            for hb in range(hb0, hb1):
                 for b2 in range(2):
-                    log_of(bp, b2, 8 * blk, 8)
-                finish(bp, blk)
-                if blk % 2 == 1:
-                    store(bp, 8 * (blk - 1), 16)
+                    v = sum_view(16 * bp + 2 * hb + b2)
+                    nc.scalar.activation(out=v, in_=v, func=ACT.Ln)
+                finish(bp, hb)
+                if hb % 2 == 1:
+                    store(bp, 4 * (hb - 1), 8)
 
         t1_done = 0
         e1_done = 0
         for n in range(-LEAD, UNITS + 5):
-            if n < PHASE2_AT:
-                target = rows_needed(max(n + LEAD + 2, 0))
-                for idx in range(t1_done, target):
-                    t1(idx)
-                t1_done = max(t1_done, target)
-                target = rows_needed(max(n + LEAD + 1, 0))
-                for idx in range(e1_done, target):
-                    e1_rows(idx)
-                e1_done = max(e1_done, target)
-            if n == PHASE2_AT:
-                for idx in range(e1_done, 2 * NI):
-                    if idx >= t1_done:
-                        t1(idx)
-                    e1_rows(idx)
+            target = 2 * YH if n >= PHASE2_AT else rows_needed(max(n + LEAD + 1, 0))
+            while e1_done < target:
+                while t1_done < min(e1_done + 2, 2 * YH):
+                    t1(t1_done)
+                    t1_done += 1
+                e1_rows(e1_done)
+                e1_done += 1
             if 0 <= n < UNITS:
                 t2(n)
                 cpo(n)
@@ -415,10 +387,13 @@ def tile_mex_kernel(tc, x, offsets, out):
                 else:
                     log_acc(gi)
                     if gi % 2 == 1:
-                        blk = (gi % 16) // 2
-                        finish(1, blk)
-                        store(1, 8 * blk, 8)
-            if n >= BG_START and background:
+                        hb = (gi % 16) // 2
+                        finish(1, hb)
+                        store(1, 4 * hb, 4)
+            for key, at in PREPARE_AT.items():
+                if n == at:
+                    background = background + prepare_tasks(key[0], key[1])
+            if background:
                 task = background[0]
                 task()
                 background = background[1:]

@@ -23,12 +23,17 @@ WO = 64
 K = 1024
 HH = 32
 YH = HH + 3
+GAP = 1
+TPH = 1
 UNITS = 128
-LEAD = 6
-PHASE1_AT = 68
-PHASE2_AT = 116
-PREPARE_AT = {(0, 1): -4, (0, 2): 14, (1, 0): 26, (1, 1): 44, (1, 2): 70}
-CHUNKS = ((0, 12), (12, 24), (24, YH))
+LEAD = 9
+QLAG = 4
+MLAG = 8
+ALAG = 9
+PHASE2_GI = 28
+PHASE2_AT = 4 * PHASE2_GI - 1 + ALAG
+PREPARE_AT = {(0, 1): -9, (0, 2): 10, (1, 0): 26, (1, 1): 46, (1, 2): 68}
+CHUNKS = ((0, 14), (14, 26), (26, YH))
 
 
 def tile_mex_kernel(tc, x, offsets, out):
@@ -38,9 +43,9 @@ def tile_mex_kernel(tc, x, offsets, out):
         const = ctx.enter_context(tc.tile_pool(name="const", bufs=1))
         rawp = ctx.enter_context(tc.tile_pool(name="raw", bufs=1))
         winp = ctx.enter_context(tc.tile_pool(name="win", bufs=2))
-        e1p = ctx.enter_context(tc.tile_pool(name="e1", bufs=32))
-        epool = ctx.enter_context(tc.tile_pool(name="ex", bufs=6))
-        gpool = ctx.enter_context(tc.tile_pool(name="grouped", bufs=2))
+        e1p = ctx.enter_context(tc.tile_pool(name="e1", bufs=40))
+        epool = ctx.enter_context(tc.tile_pool(name="ex", bufs=10))
+        gpool = ctx.enter_context(tc.tile_pool(name="grouped", bufs=3))
         cpool = ctx.enter_context(tc.tile_pool(name="codes", bufs=2))
         spool = ctx.enter_context(tc.tile_pool(name="sums", bufs=1))
         ps_x1 = ctx.enter_context(tc.psum_pool(name="ps_x1", bufs=2))
@@ -62,7 +67,7 @@ def tile_mex_kernel(tc, x, offsets, out):
 
         def load_chunk(bp, ci):
             y0, y1 = CHUNKS[ci]
-            raw[(bp, ci)] = rawp.tile([P, 2, 816], BF16, name="raw%d_%d" % (bp, ci))
+            raw[(bp, ci)] = rawp.tile([P, 2, 944], BF16, name="raw%d_%d" % (bp, ci))
             for q in range(2):
                 nc.sync.dma_start(
                     out=raw[(bp, ci)][:, q, 0 : W * (y1 - y0)],
@@ -133,7 +138,7 @@ def tile_mex_kernel(tc, x, offsets, out):
                 )
 
             def window1():
-                a1 = winp.tile([P, 134 * 12], BF16, name="a1")
+                a1 = winp.tile([P, 134 * 14], BF16, name="a1")
                 n = 134 * rows - 2
                 nc.vector.tensor_tensor(
                     out=a1[:, 0:n],
@@ -144,27 +149,34 @@ def tile_mex_kernel(tc, x, offsets, out):
                 state["a1"] = a1
 
             def window2():
-                a2 = winp.tile([P, 12, P], BF16, name="a2")
+                a2 = winp.tile([P, 14, P], BF16, name="a2")
                 v = state["a1"][:, 0 : 134 * rows].rearrange("p (y f) -> p y f", y=rows)
                 nc.vector.tensor_tensor(
                     out=a2[:, 0:rows, :], in0=v[:, :, 0:128], in1=v[:, :, 4:132], op=ALU.max
                 )
                 state["a2"] = a2
 
-            def channel_max(part):
-                def run():
-                    r0, r1 = (0, min(rows, 8)) if part == 0 else (8, rows)
+            def channel_rows(part):
+                r0, r1 = (0, min(rows, 8)) if part == 0 else (8, rows)
+
+                def turn():
                     t = ps_mb.tile([P, 8, P], BF16, tag="mb", name="hm_ps")
                     for r in range(r0, r1):
                         nc.tensor.transpose(t[:, r - r0, :], state["a2"][:, r, :], ident[:])
+                    state["t"] = t
+
+                def reduce():
                     nc.vector.tensor_reduce(
                         out=hm[bp][:, :, y0 + r0 : y0 + r1].rearrange("p b y -> p y b"),
-                        in_=t[:, 0 : r1 - r0, :].rearrange("p y (b c) -> p y b c", b=2),
+                        in_=state["t"][:, 0 : r1 - r0, :].rearrange("p y (b c) -> p y b c", b=2),
                         axis=mybir.AxisListType.X,
                         op=ALU.max,
                     )
 
-                return run
+                return turn, reduce
+
+            turn0, reduce0 = channel_rows(0)
+            turn1, reduce1 = channel_rows(1)
 
             def position_max():
                 nc.vector.tensor_scalar(
@@ -193,7 +205,19 @@ def tile_mex_kernel(tc, x, offsets, out):
                     func=ACT.Exp,
                 )
 
-            return [interleave, window1, window2, channel_max(0), channel_max(1), position_max, ratios]
+            return (
+                [interleave, window1, window2]
+                + [None] * GAP
+                + [turn0]
+                + [None] * GAP
+                + [reduce0]
+                + [None] * GAP
+                + [turn1]
+                + [None] * GAP
+                + [reduce1, position_max]
+                + [None] * GAP
+                + [ratios]
+            )
 
         def make_m(bp, hb):
             t = ps_mb.tile([P, 8, P], BF16, tag="mb", name="m_bc")
@@ -203,7 +227,8 @@ def tile_mex_kernel(tc, x, offsets, out):
             return t
 
         for task in prepare_tasks(0, 0):
-            task()
+            if task:
+                task()
         eb_tasks()
         nc.vector.quantize_mx(
             out=eb_codes[:].bitcast(FP8X4),
@@ -229,19 +254,16 @@ def tile_mex_kernel(tc, x, offsets, out):
             b2, j = divmod(r, 4)
             return bp, b2, 4 * hb + j
 
-        def rows_needed(n):
-            bp, b2, h = unit(min(n, UNITS - 1))
-            return YH * bp + h + 4
-
         x1_t = {}
 
-        def t1(idx):
-            bp, y = divmod(idx, YH)
-            x1 = ps_x1.tile([P, 4, P], BF16, name="x1")
-            for dw in range(4):
-                f = 134 * y + 2 * dw
-                nc.tensor.transpose(x1[:, dw, :], xi[bp][:, f : f + P], perm[:])
-            x1_t[idx] = x1
+        def t1(i):
+            x1 = ps_x1.tile([P, 2, 4, P], BF16, name="x1")
+            for k in range(2):
+                bp, y = divmod(2 * i + k, YH)
+                for dw in range(4):
+                    f = 134 * y + 2 * dw
+                    nc.tensor.transpose(x1[:, k, dw, :], xi[bp][:, f : f + P], perm[:])
+            x1_t[i] = x1
 
         def e1_rows(idx):
             bp, y = divmod(idx, YH)
@@ -249,7 +271,7 @@ def tile_mex_kernel(tc, x, offsets, out):
                 e1 = e1p.tile([P, 256], F32, name="e1")
                 nc.scalar.activation(
                     out=e1[:].rearrange("p (c d) -> p c d", d=4),
-                    in_=x1_t[idx][:, :, 64 * b2 : 64 * b2 + 64].rearrange("p d c -> p c d"),
+                    in_=x1_t[idx // 2][:, idx % 2, :, 64 * b2 : 64 * b2 + 64].rearrange("p d c -> p c d"),
                     func=ACT.Exp,
                     bias=neg_hm[bp][:, b2, y : y + 1],
                     scale=1.0,
@@ -362,28 +384,36 @@ def tile_mex_kernel(tc, x, offsets, out):
 
         t1_done = 0
         e1_done = 0
-        for n in range(-LEAD, UNITS + 5):
-            target = 2 * YH if n >= PHASE2_AT else rows_needed(max(n + LEAD + 1, 0))
+        for n in range(-LEAD, UNITS + 4 + ALAG):
+            u = n + LEAD
+            target = min(2 * YH, 7 + u // 2 + min(max((u - 40) // 4, 0), 3))
             while e1_done < target:
-                while t1_done < min(e1_done + 2, 2 * YH):
+                while t1_done < min(e1_done // 2 + 1, YH):
                     t1(t1_done)
                     t1_done += 1
                 e1_rows(e1_done)
                 e1_done += 1
+            if (n + LEAD) % 4 == TPH and t1_done < YH:
+                t1(t1_done)
+                t1_done += 1
             if 0 <= n < UNITS:
                 t2(n)
                 cpo(n)
-            if n % 4 == 3 and 3 <= n < UNITS:
-                quant(n // 4)
+            if (n - 3 - QLAG) % 4 == 0 and 0 <= n - 3 - QLAG < UNITS:
+                quant((n - 3 - QLAG) // 4)
             if 0 <= n + LEAD < UNITS:
                 mult(n + LEAD)
-            if n % 4 == 3 and n >= 7 and (n - 7) // 4 < 32:
-                mx((n - 7) // 4, 0)
-                mx((n - 7) // 4, 1)
-            if n % 4 == 0 and n >= 8:
-                gi = (n - 8) // 4
-                if n <= PHASE2_AT:
+            if (n - 3 - MLAG) % 4 == 0 and 0 <= n - 3 - MLAG < UNITS:
+                mx((n - 3 - MLAG) // 4, 0)
+                mx((n - 3 - MLAG) // 4, 1)
+            if (n - 3 - ALAG) % 4 == 0 and 0 <= n - 3 - ALAG < UNITS:
+                gi = (n - 3 - ALAG) // 4
+                if gi < PHASE2_GI:
                     acc_copy(gi)
+                    if gi == 15:
+                        phase(0, 0, 8)
+                    if gi == PHASE2_GI - 1:
+                        phase(1, 0, (gi - 15) // 2)
                 else:
                     log_acc(gi)
                     if gi % 2 == 1:
@@ -394,10 +424,6 @@ def tile_mex_kernel(tc, x, offsets, out):
                 if n == at:
                     background = background + prepare_tasks(key[0], key[1])
             if background:
-                task = background[0]
-                task()
+                if background[0]:
+                    background[0]()
                 background = background[1:]
-            if n == PHASE1_AT:
-                phase(0, 0, 8)
-            if n == PHASE2_AT:
-                phase(1, 0, 6)

@@ -23,17 +23,24 @@ WO = 64
 K = 1024
 HH = 32
 YH = HH + 3
-GAP = 1
-TPH = 1
 UNITS = 128
 LEAD = 9
+LEAD0 = 5
 QLAG = 4
-MLAG = 8
-ALAG = 9
-PHASE2_GI = 28
-PHASE2_AT = 4 * PHASE2_GI - 1 + ALAG
-PREPARE_AT = {(0, 1): -9, (0, 2): 10, (1, 0): 26, (1, 1): 46, (1, 2): 68}
-CHUNKS = ((0, 14), (14, 26), (26, YH))
+MLAG = 7
+ALAG = 8
+GAP = 1
+TPH = 1
+RATE0 = 6
+RATE = 2
+RATE_TO = 8
+EB_AT = 2
+SXM = 8
+PREPARE_AT = {(0, 2): 3, (1, 0): 26, (1, 1): 44, (1, 2): 64}
+CHUNKS = ((0, 8), (8, 20), (20, YH))
+CHUNKS1 = ((0, 12), (12, 24), (24, YH))
+ROWS = 16
+RAW = 1088
 
 
 def tile_mex_kernel(tc, x, offsets, out):
@@ -41,8 +48,9 @@ def tile_mex_kernel(tc, x, offsets, out):
     with ExitStack() as ctx:
         ctx.enter_context(tc.manual_schedule())
         const = ctx.enter_context(tc.tile_pool(name="const", bufs=1))
-        rawp = ctx.enter_context(tc.tile_pool(name="raw", bufs=1))
-        winp = ctx.enter_context(tc.tile_pool(name="win", bufs=2))
+        rawp = ctx.enter_context(tc.tile_pool(name="raw", bufs=4))
+        xip = ctx.enter_context(tc.tile_pool(name="xi", bufs=1))
+        winp = ctx.enter_context(tc.tile_pool(name="win", bufs=1))
         e1p = ctx.enter_context(tc.tile_pool(name="e1", bufs=40))
         epool = ctx.enter_context(tc.tile_pool(name="ex", bufs=10))
         gpool = ctx.enter_context(tc.tile_pool(name="grouped", bufs=3))
@@ -66,8 +74,8 @@ def tile_mex_kernel(tc, x, offsets, out):
         raw = {}
 
         def load_chunk(bp, ci):
-            y0, y1 = CHUNKS[ci]
-            raw[(bp, ci)] = rawp.tile([P, 2, 944], BF16, name="raw%d_%d" % (bp, ci))
+            y0, y1 = (CHUNKS, CHUNKS1)[bp][ci]
+            raw[(bp, ci)] = rawp.tile([P, 2, RAW], BF16, name="raw")
             for q in range(2):
                 nc.sync.dma_start(
                     out=raw[(bp, ci)][:, q, 0 : W * (y1 - y0)],
@@ -75,9 +83,10 @@ def tile_mex_kernel(tc, x, offsets, out):
                 )
 
         load_chunk(0, 0)
+        load_chunk(0, 1)
         offs = const.tile([P, K], BF16, name="offs")
         nc.sync.dma_start(out=offs[:], in_=offsets[0].rearrange("m c i j -> m (c i j)"))
-        for bp, ci in ((0, 1), (0, 2), (1, 0), (1, 1), (1, 2)):
+        for bp, ci in [(0, c) for c in range(2, len(CHUNKS))] + [(1, c) for c in range(len(CHUNKS1))]:
             load_chunk(bp, ci)
 
         mb = const.tile([P, 1], F32, name="mb")
@@ -89,26 +98,41 @@ def tile_mex_kernel(tc, x, offsets, out):
         eb_codes = const.tile([P, 2 * P], U32, name="eb_codes", align_bytes=64)
         eb_scales = const.tile([P, 2 * P], U8, name="eb_scales", align_bytes=64)
 
-        def eb_tasks():
+        eb = {}
+
+        def eb_exp():
             nc.vector.tensor_reduce(out=mb[:], in_=offs[:], axis=mybir.AxisListType.X, op=ALU.max)
             nc.vector.tensor_scalar(out=neg_mb[:], in0=mb[:], scalar1=-1.0, scalar2=None, op0=ALU.mult)
             nc.vector.tensor_scalar(out=cb[:], in0=mb[:], scalar1=-math.log(float(K)), scalar2=None, op0=ALU.add)
             nc.scalar.activation(
                 out=eb_n[:].rearrange("m c d w -> m (c d w)"), in_=offs[:], func=ACT.Exp, bias=neg_mb[:, 0:1], scale=1.0
             )
+
+        def eb_order():
             for dh in range(4):
                 for a in range(2):
                     nc.vector.tensor_copy(
                         out=eb_t[:, dh, 32 * a : 32 * a + 32, :].rearrange("m (g i e) w -> m g i e w", g=4, i=4, e=2),
                         in_=eb_n[:, 32 * a : 32 * a + 32, dh, :].rearrange("m (i g e) w -> m g i e w", i=4, g=4, e=2),
                     )
+
+        def eb_turn():
             eb_w = eb_t[:].rearrange("m d c w -> m (d c w)").bitcast(F32)
-            eb_ps = ps_mb.tile([P, 4, P], F32, tag="mb", name="eb_ps")
+            eb["ps"] = ps_mb.tile([P, 4, P], F32, tag="mb", name="eb_ps")
             for dh in range(4):
-                nc.tensor.transpose(eb_ps[:, dh, :], eb_w[:, P * dh : P * dh + P], ident_f[:])
+                nc.tensor.transpose(eb["ps"][:, dh, :], eb_w[:, P * dh : P * dh + P], ident_f[:])
+
+        def eb_copy():
             nc.vector.tensor_copy(
                 out=eb_g[:].rearrange("q s m t -> q (s m t)").bitcast(F32).rearrange("q (s m u) -> q s m u", s=2, m=P, u=2),
-                in_=eb_ps[:].rearrange("q (s u) m -> q s m u", s=2, u=2),
+                in_=eb["ps"][:].rearrange("q (s u) m -> q s m u", s=2, u=2),
+            )
+
+        def eb_quant():
+            nc.vector.quantize_mx(
+                out=eb_codes[:].bitcast(FP8X4),
+                scales=eb_scales[:],
+                in_=eb_g[:].rearrange("q s m t -> q (s m t)"),
             )
 
         xi = {}
@@ -118,7 +142,7 @@ def tile_mex_kernel(tc, x, offsets, out):
         r_arg = {}
         r_t = {}
         for bp in range(2):
-            xi[bp] = rawp.tile([P, YH * W * 2], BF16, name="xi%d" % bp)
+            xi[bp] = xip.tile([P, YH * W * 2], BF16, name="xi%d" % bp)
             hm[bp] = const.tile([P, 2, YH], BF16, name="hm%d" % bp)
             neg_hm[bp] = const.tile([P, 2, YH], F32, name="neg_hm%d" % bp)
             m_t[bp] = const.tile([P, 2, HH], BF16, name="m_t%d" % bp)
@@ -126,7 +150,7 @@ def tile_mex_kernel(tc, x, offsets, out):
             r_t[bp] = const.tile([P, 2, HH, 4], F32, name="r_t%d" % bp)
 
         def prepare_tasks(bp, ci):
-            y0, y1 = CHUNKS[ci]
+            y0, y1 = (CHUNKS, CHUNKS1)[bp][ci]
             rows = y1 - y0
             h0, h1 = max(y0 - 3, 0), y1 - 3
             state = {}
@@ -138,7 +162,7 @@ def tile_mex_kernel(tc, x, offsets, out):
                 )
 
             def window1():
-                a1 = winp.tile([P, 134 * 14], BF16, name="a1")
+                a1 = winp.tile([P, 134 * ROWS], BF16, name="a1")
                 n = 134 * rows - 2
                 nc.vector.tensor_tensor(
                     out=a1[:, 0:n],
@@ -149,7 +173,7 @@ def tile_mex_kernel(tc, x, offsets, out):
                 state["a1"] = a1
 
             def window2():
-                a2 = winp.tile([P, 14, P], BF16, name="a2")
+                a2 = winp.tile([P, ROWS, P], BF16, name="a2")
                 v = state["a1"][:, 0 : 134 * rows].rearrange("p (y f) -> p y f", y=rows)
                 nc.vector.tensor_tensor(
                     out=a2[:, 0:rows, :], in0=v[:, :, 0:128], in1=v[:, :, 4:132], op=ALU.max
@@ -176,13 +200,13 @@ def tile_mex_kernel(tc, x, offsets, out):
                 return turn, reduce
 
             turn0, reduce0 = channel_rows(0)
-            turn1, reduce1 = channel_rows(1)
+            turn1, reduce1 = channel_rows(1) if rows > 8 else (None, None)
 
             def position_max():
                 nc.vector.tensor_scalar(
                     out=neg_hm[bp][:, :, y0:y1], in0=hm[bp][:, :, y0:y1], scalar1=-1.0, scalar2=None, op0=ALU.mult
                 )
-                v1 = winp.tile([P, 2, 16], BF16, name="v1")
+                v1 = winp.tile([P, 2, 20], BF16, name="v1")
                 n = h1 - h0
                 nc.vector.tensor_tensor(
                     out=v1[:, :, 0 : n + 2], in0=hm[bp][:, :, h0 : h1 + 2], in1=hm[bp][:, :, h0 + 1 : h1 + 3], op=ALU.max
@@ -205,19 +229,9 @@ def tile_mex_kernel(tc, x, offsets, out):
                     func=ACT.Exp,
                 )
 
-            return (
-                [interleave, window1, window2]
-                + [None] * GAP
-                + [turn0]
-                + [None] * GAP
-                + [reduce0]
-                + [None] * GAP
-                + [turn1]
-                + [None] * GAP
-                + [reduce1, position_max]
-                + [None] * GAP
-                + [ratios]
-            )
+            gap = [None] * GAP
+            second = gap + [turn1] + gap + [reduce1] if rows > 8 else []
+            return [interleave, window1, window2] + gap + [turn0] + gap + [reduce0] + second + [position_max] + gap + [ratios]
 
         def make_m(bp, hb):
             t = ps_mb.tile([P, 8, P], BF16, tag="mb", name="m_bc")
@@ -229,14 +243,10 @@ def tile_mex_kernel(tc, x, offsets, out):
         for task in prepare_tasks(0, 0):
             if task:
                 task()
-        eb_tasks()
-        nc.vector.quantize_mx(
-            out=eb_codes[:].bitcast(FP8X4),
-            scales=eb_scales[:],
-            in_=eb_g[:].rearrange("q s m t -> q (s m t)"),
-        )
-
-        background = []
+        second = prepare_tasks(0, 1)
+        for task in second[:3]:
+            task()
+        background = second[3 + GAP :]
 
         sums = {}
         for bp in range(2):
@@ -282,7 +292,7 @@ def tile_mex_kernel(tc, x, offsets, out):
             bp, b2, h = unit(n)
             ex = epool.tile([P, K], BF16, name="ex")
             for dh in range(4):
-                if dh == 3 and n % 8 == 3:
+                if dh == 3 and n % SXM == 3:
                     nc.scalar.activation(
                         out=ex[:, 256 * dh : 256 * dh + 256],
                         in_=e1_t[(bp, b2, h + dh)][:],
@@ -352,19 +362,6 @@ def tile_mex_kernel(tc, x, offsets, out):
         def log_acc(gi):
             nc.scalar.activation(out=sum_view(gi), in_=acc_view(gi), func=ACT.Ln)
 
-        def finish(bp, hb):
-            m_bc = make_m(bp, hb)
-            for b2 in range(2):
-                v = sum_view(16 * bp + 2 * hb + b2)
-                nc.vector.scalar_tensor_tensor(
-                    out=v,
-                    in0=v,
-                    scalar=cb[:, 0:1],
-                    in1=m_bc[:, 4 * b2 : 4 * b2 + 4, :].rearrange("p h (w q) -> p q (h w)", q=2),
-                    op0=ALU.add,
-                    op1=ALU.add,
-                )
-
         def store(bp, r0, rows):
             for b2 in range(2):
                 for q in range(2):
@@ -373,27 +370,50 @@ def tile_mex_kernel(tc, x, offsets, out):
                         in_=sums[bp][:, b2, q, r0 : r0 + rows, :].rearrange("m h w -> m (h w)"),
                     )
 
-        def phase(bp, hb0, hb1):
-            for hb in range(hb0, hb1):
-                for b2 in range(2):
-                    v = sum_view(16 * bp + 2 * hb + b2)
-                    nc.scalar.activation(out=v, in_=v, func=ACT.Ln)
-                finish(bp, hb)
-                if hb % 2 == 1:
-                    store(bp, 4 * (hb - 1), 8)
+        to_log = []
+        logged = []
+        to_finish = []
+
+        def log_sum(gi):
+            v = sum_view(gi)
+            nc.scalar.activation(out=v, in_=v, func=ACT.Ln)
+
+        def phase(groups):
+            for i in range(0, len(groups), 2):
+                pair = groups[i : i + 2]
+                for gi in pair:
+                    log_sum(gi)
+                m_bc = make_m(pair[0] // 16, pair[0] % 16 // 2)
+                for gi in pair:
+                    finish_group(gi, m_bc)
+                if pair[-1] % 4 == 3:
+                    store(pair[0] // 16, 8 * (pair[0] % 16 // 4), 8)
+
+        def finish_group(gi, m_bc):
+            b2 = gi % 2
+            v = sum_view(gi)
+            nc.vector.scalar_tensor_tensor(
+                out=v,
+                in0=v,
+                scalar=cb[:, 0:1],
+                in1=m_bc[:, 4 * b2 : 4 * b2 + 4, :].rearrange("p h (w q) -> p q (h w)", q=2),
+                op0=ALU.add,
+                op1=ALU.add,
+            )
 
         t1_done = 0
         e1_done = 0
-        for n in range(-LEAD, UNITS + 4 + ALAG):
-            u = n + LEAD
-            target = min(2 * YH, 7 + u // 2 + min(max((u - 40) // 4, 0), 3))
+        mults = 0
+        for n in range(-LEAD0, UNITS + 6 + ALAG):
+            u = n + min(LEAD, LEAD0 + max(n, 0) // 2)
+            target = min(2 * YH, 5 + u, 7 + u // 2 + min(max((u - 40) // 4, 0), 3))
             while e1_done < target:
                 while t1_done < min(e1_done // 2 + 1, YH):
                     t1(t1_done)
                     t1_done += 1
                 e1_rows(e1_done)
                 e1_done += 1
-            if (n + LEAD) % 4 == TPH and t1_done < YH:
+            if u % 4 == TPH and t1_done < YH and t1_done <= e1_done // 2 + 1 and u > 8:
                 t1(t1_done)
                 t1_done += 1
             if 0 <= n < UNITS:
@@ -401,29 +421,44 @@ def tile_mex_kernel(tc, x, offsets, out):
                 cpo(n)
             if (n - 3 - QLAG) % 4 == 0 and 0 <= n - 3 - QLAG < UNITS:
                 quant((n - 3 - QLAG) // 4)
-            if 0 <= n + LEAD < UNITS:
-                mult(n + LEAD)
+            while mults < min(UNITS, u + 1):
+                mult(mults)
+                mults += 1
             if (n - 3 - MLAG) % 4 == 0 and 0 <= n - 3 - MLAG < UNITS:
                 mx((n - 3 - MLAG) // 4, 0)
                 mx((n - 3 - MLAG) // 4, 1)
+            for gi, m_bc, last in to_finish:
+                finish_group(gi, m_bc)
+                if last:
+                    store(gi // 16, 8 * (gi % 16 // 4), 8)
+            to_finish = []
             if (n - 3 - ALAG) % 4 == 0 and 0 <= n - 3 - ALAG < UNITS:
                 gi = (n - 3 - ALAG) // 4
-                if gi < PHASE2_GI:
+                if e1_done < 2 * YH:
                     acc_copy(gi)
-                    if gi == 15:
-                        phase(0, 0, 8)
-                    if gi == PHASE2_GI - 1:
-                        phase(1, 0, (gi - 15) // 2)
+                    to_log.append(gi)
                 else:
                     log_acc(gi)
-                    if gi % 2 == 1:
-                        hb = (gi % 16) // 2
-                        finish(1, hb)
-                        store(1, 4 * hb, 4)
+                    logged.append(gi)
+            if to_log and e1_done == 2 * YH:
+                even = len(to_log) // 2 * 2
+                phase(to_log[:even])
+                for gi in to_log[even:]:
+                    log_sum(gi)
+                logged = to_log[even:] + logged
+                to_log = []
+            while len(logged) >= 2:
+                m_bc = make_m(logged[0] // 16, logged[0] % 16 // 2)
+                for gi in logged[:2]:
+                    to_finish.append((gi, m_bc, gi % 4 == 3))
+                logged = logged[2:]
             for key, at in PREPARE_AT.items():
                 if n == at:
                     background = background + prepare_tasks(key[0], key[1])
-            if background:
-                if background[0]:
-                    background[0]()
-                background = background[1:]
+            if n == EB_AT:
+                background = [eb_exp, eb_order, None, eb_turn, None, eb_copy, eb_quant] + background
+            for i in range(RATE0 if n < -2 else RATE if n < RATE_TO else 1):
+                if background:
+                    if background[0]:
+                        background[0]()
+                    background = background[1:]

@@ -26,17 +26,22 @@ YH = HH + 3
 UNITS = 128
 LEAD = 9
 LEAD0 = 5
-QLAG = 4
-MLAG = 7
-ALAG = 8
+QLAG = 5
+MLAG = 8
+ALAG = 9
 GAP = 1
-TPH = 1
+PER = 4
+UOFF = 8
+TLAG = 3
+NLOG = 2
+FINN = 1
+DELAY = 3
 RATE0 = 6
 RATE = 2
 RATE_TO = 8
 EB_AT = 2
 SXM = 8
-PREPARE_AT = {(0, 2): 3, (1, 0): 26, (1, 1): 44, (1, 2): 64}
+PREPARE_AT = {(0, 2): 0, (1, 0): 26, (1, 1): 44, (1, 2): 64}
 CHUNKS = ((0, 8), (8, 20), (20, YH))
 CHUNKS1 = ((0, 12), (12, 24), (24, YH))
 ROWS = 16
@@ -51,7 +56,7 @@ def tile_mex_kernel(tc, x, offsets, out):
         rawp = ctx.enter_context(tc.tile_pool(name="raw", bufs=4))
         xip = ctx.enter_context(tc.tile_pool(name="xi", bufs=1))
         winp = ctx.enter_context(tc.tile_pool(name="win", bufs=1))
-        e1p = ctx.enter_context(tc.tile_pool(name="e1", bufs=40))
+        e1p = ctx.enter_context(tc.tile_pool(name="e1", bufs=60))
         epool = ctx.enter_context(tc.tile_pool(name="ex", bufs=10))
         gpool = ctx.enter_context(tc.tile_pool(name="grouped", bufs=3))
         cpool = ctx.enter_context(tc.tile_pool(name="codes", bufs=2))
@@ -83,9 +88,9 @@ def tile_mex_kernel(tc, x, offsets, out):
                 )
 
         load_chunk(0, 0)
-        load_chunk(0, 1)
         offs = const.tile([P, K], BF16, name="offs")
         nc.sync.dma_start(out=offs[:], in_=offsets[0].rearrange("m c i j -> m (c i j)"))
+        load_chunk(0, 1)
         for bp, ci in [(0, c) for c in range(2, len(CHUNKS))] + [(1, c) for c in range(len(CHUNKS1))]:
             load_chunk(bp, ci)
 
@@ -100,10 +105,12 @@ def tile_mex_kernel(tc, x, offsets, out):
 
         eb = {}
 
-        def eb_exp():
+        def eb_max():
             nc.vector.tensor_reduce(out=mb[:], in_=offs[:], axis=mybir.AxisListType.X, op=ALU.max)
             nc.vector.tensor_scalar(out=neg_mb[:], in0=mb[:], scalar1=-1.0, scalar2=None, op0=ALU.mult)
             nc.vector.tensor_scalar(out=cb[:], in0=mb[:], scalar1=-math.log(float(K)), scalar2=None, op0=ALU.add)
+
+        def eb_exp():
             nc.scalar.activation(
                 out=eb_n[:].rearrange("m c d w -> m (c d w)"), in_=offs[:], func=ACT.Exp, bias=neg_mb[:, 0:1], scale=1.0
             )
@@ -203,7 +210,8 @@ def tile_mex_kernel(tc, x, offsets, out):
             turn1, reduce1 = channel_rows(1) if rows > 8 else (None, None)
 
             def position_max():
-                nc.vector.tensor_scalar(
+                side = nc.gpsimd if (bp, ci) > (0, 1) else nc.vector
+                side.tensor_scalar(
                     out=neg_hm[bp][:, :, y0:y1], in0=hm[bp][:, :, y0:y1], scalar1=-1.0, scalar2=None, op0=ALU.mult
                 )
                 v1 = winp.tile([P, 2, 20], BF16, name="v1")
@@ -215,7 +223,7 @@ def tile_mex_kernel(tc, x, offsets, out):
                     out=m_t[bp][:, :, h0:h1], in0=v1[:, :, 0:n], in1=v1[:, :, 2 : n + 2], op=ALU.max
                 )
                 for dh in range(4):
-                    nc.vector.tensor_tensor(
+                    side.tensor_tensor(
                         out=r_arg[bp][:, :, h0:h1, dh],
                         in0=hm[bp][:, :, h0 + dh : h1 + dh],
                         in1=m_t[bp][:, :, h0:h1],
@@ -233,18 +241,19 @@ def tile_mex_kernel(tc, x, offsets, out):
             second = gap + [turn1] + gap + [reduce1] if rows > 8 else []
             return [interleave, window1, window2] + gap + [turn0] + gap + [reduce0] + second + [position_max] + gap + [ratios]
 
+        made = []
+
         def make_m(bp, hb):
-            t = ps_mb.tile([P, 8, P], BF16, tag="mb", name="m_bc")
+            made.append(0)
+            t = (ps_mb, ps_x1)[len(made) % 2].tile([P, 2, 4, P], BF16, tag=("mb", "x1")[len(made) % 2], name="m_bc")
             for r in range(8):
                 h = 4 * hb + r % 4
-                nc.tensor.transpose(t[:, r, :], m_t[bp][:, r // 4, h : h + 1].to_broadcast([P, P]), ident[:])
+                nc.tensor.transpose(t[:, r // 4, r % 4, :], m_t[bp][:, r // 4, h : h + 1].to_broadcast([P, P]), ident[:])
             return t
 
-        for task in prepare_tasks(0, 0):
-            if task:
-                task()
+        first = [task for task in prepare_tasks(0, 0) if task]
         second = prepare_tasks(0, 1)
-        for task in second[:3]:
+        for task in first[:4] + [eb_max, eb_exp] + first[4:6] + second[:1] + first[6:] + second[1:3] + [eb_order]:
             task()
         background = second[3 + GAP :]
 
@@ -267,7 +276,7 @@ def tile_mex_kernel(tc, x, offsets, out):
         x1_t = {}
 
         def t1(i):
-            x1 = ps_x1.tile([P, 2, 4, P], BF16, name="x1")
+            x1 = ps_x1.tile([P, 2, 4, P], BF16, tag="x1", name="x1")
             for k in range(2):
                 bp, y = divmod(2 * i + k, YH)
                 for dw in range(4):
@@ -378,17 +387,6 @@ def tile_mex_kernel(tc, x, offsets, out):
             v = sum_view(gi)
             nc.scalar.activation(out=v, in_=v, func=ACT.Ln)
 
-        def phase(groups):
-            for i in range(0, len(groups), 2):
-                pair = groups[i : i + 2]
-                for gi in pair:
-                    log_sum(gi)
-                m_bc = make_m(pair[0] // 16, pair[0] % 16 // 2)
-                for gi in pair:
-                    finish_group(gi, m_bc)
-                if pair[-1] % 4 == 3:
-                    store(pair[0] // 16, 8 * (pair[0] % 16 // 4), 8)
-
         def finish_group(gi, m_bc):
             b2 = gi % 2
             v = sum_view(gi)
@@ -396,24 +394,26 @@ def tile_mex_kernel(tc, x, offsets, out):
                 out=v,
                 in0=v,
                 scalar=cb[:, 0:1],
-                in1=m_bc[:, 4 * b2 : 4 * b2 + 4, :].rearrange("p h (w q) -> p q (h w)", q=2),
+                in1=m_bc[:, b2, :, :].rearrange("p h (w q) -> p q (h w)", q=2),
                 op0=ALU.add,
                 op1=ALU.add,
             )
 
+        freed = []
         t1_done = 0
         e1_done = 0
         mults = 0
         for n in range(-LEAD0, UNITS + 6 + ALAG):
             u = n + min(LEAD, LEAD0 + max(n, 0) // 2)
-            target = min(2 * YH, 5 + u, 7 + u // 2 + min(max((u - 40) // 4, 0), 3))
+            target = min(2 * YH, 5 + u, 8 + 2 * ((u + UOFF) // PER))
+            freed.append(e1_done // 2)
             while e1_done < target:
                 while t1_done < min(e1_done // 2 + 1, YH):
                     t1(t1_done)
                     t1_done += 1
                 e1_rows(e1_done)
                 e1_done += 1
-            if u % 4 == TPH and t1_done < YH and t1_done <= e1_done // 2 + 1 and u > 8:
+            if t1_done < YH and len(freed) > TLAG and t1_done <= freed[-1 - TLAG] + 1:
                 t1(t1_done)
                 t1_done += 1
             if 0 <= n < UNITS:
@@ -427,11 +427,11 @@ def tile_mex_kernel(tc, x, offsets, out):
             if (n - 3 - MLAG) % 4 == 0 and 0 <= n - 3 - MLAG < UNITS:
                 mx((n - 3 - MLAG) // 4, 0)
                 mx((n - 3 - MLAG) // 4, 1)
-            for gi, m_bc, last in to_finish:
+            while to_finish and to_finish[0][0] <= n:
+                due, gi, m_bc = to_finish.pop(0)
                 finish_group(gi, m_bc)
-                if last:
+                if gi % 4 == 3:
                     store(gi // 16, 8 * (gi % 16 // 4), 8)
-            to_finish = []
             if (n - 3 - ALAG) % 4 == 0 and 0 <= n - 3 - ALAG < UNITS:
                 gi = (n - 3 - ALAG) // 4
                 if e1_done < 2 * YH:
@@ -440,23 +440,25 @@ def tile_mex_kernel(tc, x, offsets, out):
                 else:
                     log_acc(gi)
                     logged.append(gi)
-            if to_log and e1_done == 2 * YH:
-                even = len(to_log) // 2 * 2
-                phase(to_log[:even])
-                for gi in to_log[even:]:
+                    logged.sort()
+            if e1_done == 2 * YH:
+                some = to_log[: NLOG if n < UNITS else 99]
+                for gi in some:
                     log_sum(gi)
-                logged = to_log[even:] + logged
-                to_log = []
-            while len(logged) >= 2:
+                logged = sorted(some + logged)
+                to_log = to_log[len(some) :]
+            pairs = 0
+            while len(logged) >= 2 and logged[0] % 2 == 0 and logged[1] == logged[0] + 1 and (pairs < FINN or n >= UNITS):
+                pairs += 1
                 m_bc = make_m(logged[0] // 16, logged[0] % 16 // 2)
                 for gi in logged[:2]:
-                    to_finish.append((gi, m_bc, gi % 4 == 3))
+                    to_finish.append((n + DELAY, gi, m_bc))
                 logged = logged[2:]
             for key, at in PREPARE_AT.items():
                 if n == at:
                     background = background + prepare_tasks(key[0], key[1])
             if n == EB_AT:
-                background = [eb_exp, eb_order, None, eb_turn, None, eb_copy, eb_quant] + background
+                background = [eb_turn, None, eb_copy, eb_quant] + background
             for i in range(RATE0 if n < -2 else RATE if n < RATE_TO else 1):
                 if background:
                     if background[0]:

@@ -210,8 +210,7 @@ def tile_mex_kernel(tc, x, offsets, out):
             turn1, reduce1 = channel_rows(1) if rows > 8 else (None, None)
 
             def position_max():
-                side = nc.gpsimd if (bp, ci) > (0, 1) else nc.vector
-                side.tensor_scalar(
+                nc.vector.tensor_scalar(
                     out=neg_hm[bp][:, :, y0:y1], in0=hm[bp][:, :, y0:y1], scalar1=-1.0, scalar2=None, op0=ALU.mult
                 )
                 v1 = winp.tile([P, 2, 20], BF16, name="v1")
@@ -223,7 +222,7 @@ def tile_mex_kernel(tc, x, offsets, out):
                     out=m_t[bp][:, :, h0:h1], in0=v1[:, :, 0:n], in1=v1[:, :, 2 : n + 2], op=ALU.max
                 )
                 for dh in range(4):
-                    side.tensor_tensor(
+                    nc.vector.tensor_tensor(
                         out=r_arg[bp][:, :, h0:h1, dh],
                         in0=hm[bp][:, :, h0 + dh : h1 + dh],
                         in1=m_t[bp][:, :, h0:h1],

@@ -32,15 +32,16 @@ ALAG = 9
 GAP = 1
 PER = 4
 UOFF = 8
-TLAG = 3
+TLAG = 2
 NLOG = 2
 FINN = 1
 DELAY = 3
 RATE0 = 6
 RATE = 2
 RATE_TO = 8
-EB_AT = 2
+EB_AT = -1
 SXM = 8
+SX0 = 10
 PREPARE_AT = {(0, 2): 0, (1, 0): 26, (1, 1): 44, (1, 2): 64}
 CHUNKS = ((0, 8), (8, 20), (20, YH))
 CHUNKS1 = ((0, 12), (12, 24), (24, YH))
@@ -65,6 +66,10 @@ def tile_mex_kernel(tc, x, offsets, out):
         ps_tp = ctx.enter_context(tc.psum_pool(name="ps_tp", bufs=3))
         ps_acc = ctx.enter_context(tc.psum_pool(name="ps_acc", bufs=1))
         ps_mb = ctx.enter_context(tc.psum_pool(name="ps_mb", bufs=2))
+
+        start = const.tile([P, 1], F32, name="start")
+        nc.vector.memset(start[:], 0.0)
+        nc.scalar.activation(out=start[:], in_=start[:], func=ACT.Exp)
 
         ident = const.tile([P, P], BF16, name="ident")
         make_identity(nc, ident[:])
@@ -214,13 +219,20 @@ def tile_mex_kernel(tc, x, offsets, out):
                     out=neg_hm[bp][:, :, y0:y1], in0=hm[bp][:, :, y0:y1], scalar1=-1.0, scalar2=None, op0=ALU.mult
                 )
                 v1 = winp.tile([P, 2, 20], BF16, name="v1")
+                state["v1"] = v1
                 n = h1 - h0
                 nc.vector.tensor_tensor(
                     out=v1[:, :, 0 : n + 2], in0=hm[bp][:, :, h0 : h1 + 2], in1=hm[bp][:, :, h0 + 1 : h1 + 3], op=ALU.max
                 )
+
+            def window_max():
+                n = h1 - h0
+                v1 = state["v1"]
                 nc.vector.tensor_tensor(
                     out=m_t[bp][:, :, h0:h1], in0=v1[:, :, 0:n], in1=v1[:, :, 2 : n + 2], op=ALU.max
                 )
+
+            def differences():
                 for dh in range(4):
                     nc.vector.tensor_tensor(
                         out=r_arg[bp][:, :, h0:h1, dh],
@@ -238,7 +250,17 @@ def tile_mex_kernel(tc, x, offsets, out):
 
             gap = [None] * GAP
             second = gap + [turn1] + gap + [reduce1] if rows > 8 else []
-            return [interleave, window1, window2] + gap + [turn0] + gap + [reduce0] + second + [position_max] + gap + [ratios]
+            return (
+                [interleave, window1, window2]
+                + gap
+                + [turn0]
+                + gap
+                + [reduce0]
+                + second
+                + [position_max, window_max, differences]
+                + gap
+                + [ratios]
+            )
 
         made = []
 
@@ -252,7 +274,7 @@ def tile_mex_kernel(tc, x, offsets, out):
 
         first = [task for task in prepare_tasks(0, 0) if task]
         second = prepare_tasks(0, 1)
-        for task in first[:4] + [eb_max, eb_exp] + first[4:6] + second[:1] + first[6:] + second[1:3] + [eb_order]:
+        for task in first[:4] + [eb_max, eb_exp] + first[4:8] + second[:1] + first[8:] + second[1:3]:
             task()
         background = second[3 + GAP :]
 
@@ -300,7 +322,7 @@ def tile_mex_kernel(tc, x, offsets, out):
             bp, b2, h = unit(n)
             ex = epool.tile([P, K], BF16, name="ex")
             for dh in range(4):
-                if dh == 3 and n % SXM == 3:
+                if dh == 3 and (n % SXM == 3 or n < SX0):
                     nc.scalar.activation(
                         out=ex[:, 256 * dh : 256 * dh + 256],
                         in_=e1_t[(bp, b2, h + dh)][:],
@@ -457,7 +479,7 @@ def tile_mex_kernel(tc, x, offsets, out):
                 if n == at:
                     background = background + prepare_tasks(key[0], key[1])
             if n == EB_AT:
-                background = [eb_turn, None, eb_copy, eb_quant] + background
+                background = [eb_order, None, eb_turn, None, eb_copy, eb_quant] + background
             for i in range(RATE0 if n < -2 else RATE if n < RATE_TO else 1):
                 if background:
                     if background[0]:

@@ -39,14 +39,15 @@ DELAY = 3
 RATE0 = 6
 RATE = 2
 RATE_TO = 8
-EB_AT = -1
-SXM = 8
+EB_AT = 4
+SXM = 16
 SX0 = 10
-PREPARE_AT = {(0, 2): 0, (1, 0): 26, (1, 1): 44, (1, 2): 64}
+PREPARE_AT = {(0, 2): -2, (1, 0): 22, (1, 1): 48}
 CHUNKS = ((0, 8), (8, 20), (20, YH))
-CHUNKS1 = ((0, 12), (12, 24), (24, YH))
-ROWS = 16
-RAW = 1088
+CHUNKS1 = ((0, 15), (15, YH))
+NEW = ((False, False, True), (True, True))
+ROWS = 12
+RAW = 1344
 
 
 def tile_mex_kernel(tc, x, offsets, out):
@@ -54,7 +55,7 @@ def tile_mex_kernel(tc, x, offsets, out):
     with ExitStack() as ctx:
         ctx.enter_context(tc.manual_schedule())
         const = ctx.enter_context(tc.tile_pool(name="const", bufs=1))
-        rawp = ctx.enter_context(tc.tile_pool(name="raw", bufs=4))
+        rawp = ctx.enter_context(tc.tile_pool(name="raw", bufs=3))
         xip = ctx.enter_context(tc.tile_pool(name="xi", bufs=1))
         winp = ctx.enter_context(tc.tile_pool(name="win", bufs=1))
         e1p = ctx.enter_context(tc.tile_pool(name="e1", bufs=60))
@@ -147,6 +148,37 @@ def tile_mex_kernel(tc, x, offsets, out):
                 in_=eb_g[:].rearrange("q s m t -> q (s m t)"),
             )
 
+        xe = const.tile([P, P], BF16, name="xe")
+        pm = const.tile([P, 2, 24], BF16, name="pm")
+        pe = const.tile([P, 2, 24], BF16, name="pe")
+        mask = const.tile([P, 24], BF16, name="mask")
+        shift = const.tile([P, 3, P], BF16, name="shift")
+        ends = const.tile([P, 3, P], BF16, name="ends")
+        sixes = const.tile([P, P], BF16, name="sixes")
+        edge = const.tile([P, 3, P], BF16, name="edge")
+        for t in (xe, pm, pe, mask, shift, ends, sixes):
+            nc.vector.memset(t[:], 0.0)
+
+        def edge_tasks():
+            nc.vector.tensor_reduce(
+                out=mask[:, 0:21],
+                in_=ident[:, 0:126].rearrange("p (y f) -> p y f", f=6),
+                axis=mybir.AxisListType.X,
+                op=ALU.max,
+            )
+            nc.scalar.copy(
+                out=sixes[:, 0:126].rearrange("p (y f) -> p y f", f=6),
+                in_=ident[:, 0:6].unsqueeze(1).to_broadcast([P, 21, 6]),
+            )
+            for i in range(3):
+                n = 2 * (i + 1)
+                nc.scalar.copy(out=shift[:, i, 0 : P - n], in_=ident[:, n:P])
+                nc.scalar.copy(out=ends[:, i, P - n : P], in_=ident[:, 0:n])
+            t = ps_mb.tile([P, 3, P], F32, tag="mb", name="edge_ps")
+            for i in range(3):
+                nc.tensor.matmul(out=t[:, i, :], lhsT=sixes[:], rhs=ends[:, i, :], start=True, stop=True)
+            nc.scalar.copy(out=edge[:], in_=t[:])
+
         xi = {}
         hm = {}
         neg_hm = {}
@@ -172,6 +204,69 @@ def tile_mex_kernel(tc, x, offsets, out):
                     out=xi[bp][:, 134 * y0 : 134 * y1].rearrange("p (f q) -> p f q", q=2),
                     in_=raw[(bp, ci)][:, :, 0 : W * rows].rearrange("p q f -> p f q"),
                 )
+
+            def edges():
+                nc.vector.tensor_copy(
+                    out=xe[:, 0 : 6 * rows].rearrange("p (y f) -> p y f", f=6),
+                    in_=xi[bp][:, 134 * y0 : 134 * y1].rearrange("p (y f) -> p y f", f=134)[:, :, 128:134],
+                )
+
+            def turn_rows(s0, s1):
+                def run():
+                    t = ps_mb.tile([P, 8, P], BF16, tag="mb", name="hm_ps")
+                    for s in range(s0, s1):
+                        f = 134 * (y0 + s)
+                        nc.tensor.transpose(
+                            t[:, s - s0, :], xi[bp][:, f : f + P] if s < rows else xe[:], ident[:]
+                        )
+                    state["t"] = t
+
+                return run
+
+            def reduce_rows(s0, s1):
+                def run():
+                    nc.vector.tensor_reduce(
+                        out=pm[:, :, s0:s1].rearrange("p b y -> p y b"),
+                        in_=state["t"][:, 0 : s1 - s0, :].rearrange("p y (b c) -> p y b c", b=2),
+                        axis=mybir.AxisListType.X,
+                        op=ALU.max,
+                    )
+
+                return run
+
+            def spread():
+                for b2 in range(2):
+                    nc.vector.tensor_scalar(
+                        out=pe[:, b2, 0:rows],
+                        in0=mask[:, 0:rows],
+                        scalar1=pm[:, b2, rows : rows + 1],
+                        scalar2=None,
+                        op0=ALU.mult,
+                    )
+
+            def shift_columns():
+                sh = ps_mb.tile([P, 3, 2, 24], F32, tag="mb", name="sh")
+                for i in range(3):
+                    o = sh[:, i, :, :].rearrange("p b y -> p (b y)")
+                    nc.tensor.matmul(
+                        out=o, lhsT=shift[:, i, :], rhs=pm[:].rearrange("p b y -> p (b y)"), start=True, stop=False
+                    )
+                    nc.tensor.matmul(
+                        out=o, lhsT=edge[:, i, :], rhs=pe[:].rearrange("p b y -> p (b y)"), start=False, stop=True
+                    )
+                state["sh"] = sh
+
+            def shifted_max(i):
+                def run():
+                    last = pm[:, :, 0:rows] if i == 0 else state["w"][:, :, 0:rows]
+                    if i == 2:
+                        w = hm[bp][:, :, y0:y1]
+                    else:
+                        state["w"] = winp.tile([P, 2, 24], BF16, name="w%d" % i)
+                        w = state["w"][:, :, 0:rows]
+                    nc.vector.tensor_tensor(out=w, in0=state["sh"][:, i, :, 0:rows], in1=last, op=ALU.max)
+
+                return run
 
             def window1():
                 a1 = winp.tile([P, 134 * ROWS], BF16, name="a1")
@@ -218,7 +313,7 @@ def tile_mex_kernel(tc, x, offsets, out):
                 nc.vector.tensor_scalar(
                     out=neg_hm[bp][:, :, y0:y1], in0=hm[bp][:, :, y0:y1], scalar1=-1.0, scalar2=None, op0=ALU.mult
                 )
-                v1 = winp.tile([P, 2, 20], BF16, name="v1")
+                v1 = winp.tile([P, 2, 24], BF16, name="v1")
                 state["v1"] = v1
                 n = h1 - h0
                 nc.vector.tensor_tensor(
@@ -250,6 +345,15 @@ def tile_mex_kernel(tc, x, offsets, out):
 
             gap = [None] * GAP
             second = gap + [turn1] + gap + [reduce1] if rows > 8 else []
+            tail = [position_max, window_max, differences] + gap + [ratios]
+            if NEW[bp][ci]:
+                tasks = [interleave, edges] + gap
+                for s0 in range(0, rows + 1, 8):
+                    s1 = min(s0 + 8, rows + 1)
+                    tasks = tasks + [turn_rows(s0, s1)] + gap + [reduce_rows(s0, s1)]
+                return (
+                    tasks + [spread] + gap + [shift_columns] + gap + [shifted_max(0), shifted_max(1), shifted_max(2)] + tail
+                )
             return (
                 [interleave, window1, window2]
                 + gap
@@ -257,9 +361,7 @@ def tile_mex_kernel(tc, x, offsets, out):
                 + gap
                 + [reduce0]
                 + second
-                + [position_max, window_max, differences]
-                + gap
-                + [ratios]
+                + tail
             )
 
         made = []
@@ -272,6 +374,7 @@ def tile_mex_kernel(tc, x, offsets, out):
                 nc.tensor.transpose(t[:, r // 4, r % 4, :], m_t[bp][:, r // 4, h : h + 1].to_broadcast([P, P]), ident[:])
             return t
 
+        edge_tasks()
         first = [task for task in prepare_tasks(0, 0) if task]
         second = prepare_tasks(0, 1)
         for task in first[:4] + [eb_max, eb_exp] + first[4:8] + second[:1] + first[8:] + second[1:3]:

@@ -33,21 +33,20 @@ GAP = 1
 PER = 4
 UOFF = 8
 TLAG = 2
-NLOG = 2
-FINN = 1
-DELAY = 3
+DELAY = 4
 RATE0 = 6
 RATE = 2
 RATE_TO = 8
+EARLY = 1
 EB_AT = 4
-SXM = 16
-SX0 = 10
-PREPARE_AT = {(0, 2): -2, (1, 0): 22, (1, 1): 48}
+SXM = 32
+SX0 = 8
+PREPARE_AT = {(0, 2): -2, (1, 0): 24, (1, 1): 46}
 CHUNKS = ((0, 8), (8, 20), (20, YH))
-CHUNKS1 = ((0, 15), (15, YH))
-NEW = ((False, False, True), (True, True))
-ROWS = 12
-RAW = 1344
+CHUNKS1 = ((0, 14), (14, YH))
+NEW = ((False, True, True), (True, True))
+ROWS = 8
+RAW = 1408
 
 
 def tile_mex_kernel(tc, x, offsets, out):
@@ -58,7 +57,8 @@ def tile_mex_kernel(tc, x, offsets, out):
         rawp = ctx.enter_context(tc.tile_pool(name="raw", bufs=3))
         xip = ctx.enter_context(tc.tile_pool(name="xi", bufs=1))
         winp = ctx.enter_context(tc.tile_pool(name="win", bufs=1))
-        e1p = ctx.enter_context(tc.tile_pool(name="e1", bufs=60))
+        e1k = ctx.enter_context(tc.tile_pool(name="e1k", bufs=6))
+        e1p = ctx.enter_context(tc.tile_pool(name="e1", bufs=55))
         epool = ctx.enter_context(tc.tile_pool(name="ex", bufs=10))
         gpool = ctx.enter_context(tc.tile_pool(name="grouped", bufs=3))
         cpool = ctx.enter_context(tc.tile_pool(name="codes", bufs=2))
@@ -82,16 +82,22 @@ def tile_mex_kernel(tc, x, offsets, out):
             in_=ident[:].rearrange("p (x i g e) -> p x g i e", x=4, i=4, g=4, e=2),
         )
 
+        perm_w = const.tile([P, P], BF16, name="perm_w")
+        nc.vector.tensor_copy(
+            out=perm_w[:].rearrange("p (b w) -> p b w", b=2), in_=ident[:].rearrange("p (w b) -> p b w", b=2)
+        )
+
         raw = {}
 
         def load_chunk(bp, ci):
             y0, y1 = (CHUNKS, CHUNKS1)[bp][ci]
             raw[(bp, ci)] = rawp.tile([P, 2, RAW], BF16, name="raw")
-            for q in range(2):
-                nc.sync.dma_start(
-                    out=raw[(bp, ci)][:, q, 0 : W * (y1 - y0)],
-                    in_=x[2 * bp : 2 * bp + 2, :, HH * q + y0 : HH * q + y1, :].rearrange("b c y z -> (b c) (y z)"),
-                )
+            for b2 in range(2):
+                for q in range(2):
+                    nc.sync.dma_start(
+                        out=raw[(bp, ci)][64 * q : 64 * q + 64, b2, 0 : W * (y1 - y0)],
+                        in_=x[2 * bp + b2, :, HH * q + y0 : HH * q + y1, :].rearrange("c y z -> c (y z)"),
+                    )
 
         load_chunk(0, 0)
         offs = const.tile([P, K], BF16, name="offs")
@@ -103,7 +109,6 @@ def tile_mex_kernel(tc, x, offsets, out):
         mb = const.tile([P, 1], F32, name="mb")
         neg_mb = const.tile([P, 1], F32, name="neg_mb")
         cb = const.tile([P, 1], F32, name="cb")
-        eb_n = const.tile([P, C, 4, 4], BF16, name="eb_n")
         eb_t = const.tile([P, 4, C, 4], BF16, name="eb_t")
         eb_g = const.tile([P, 2, P, 4], BF16, name="eb_g", align_bytes=64)
         eb_codes = const.tile([P, 2 * P], U32, name="eb_codes", align_bytes=64)
@@ -117,17 +122,18 @@ def tile_mex_kernel(tc, x, offsets, out):
             nc.vector.tensor_scalar(out=cb[:], in0=mb[:], scalar1=-math.log(float(K)), scalar2=None, op0=ALU.add)
 
         def eb_exp():
-            nc.scalar.activation(
-                out=eb_n[:].rearrange("m c d w -> m (c d w)"), in_=offs[:], func=ACT.Exp, bias=neg_mb[:, 0:1], scale=1.0
-            )
-
-        def eb_order():
+            v = offs[:].rearrange("m (a i g e d w) -> m a g d i e w", a=2, i=4, g=4, e=2, d=4, w=4)
             for dh in range(4):
                 for a in range(2):
-                    nc.vector.tensor_copy(
-                        out=eb_t[:, dh, 32 * a : 32 * a + 32, :].rearrange("m (g i e) w -> m g i e w", g=4, i=4, e=2),
-                        in_=eb_n[:, 32 * a : 32 * a + 32, dh, :].rearrange("m (i g e) w -> m g i e w", i=4, g=4, e=2),
-                    )
+                    for g in range(4):
+                        c0 = 32 * a + 8 * g
+                        nc.scalar.activation(
+                            out=eb_t[:, dh, c0 : c0 + 8, :].rearrange("m (i e) w -> m i e w", e=2),
+                            in_=v[:, a, g, dh, :, :, :],
+                            func=ACT.Exp,
+                            bias=neg_mb[:, 0:1],
+                            scale=1.0,
+                        )
 
         def eb_turn():
             eb_w = eb_t[:].rearrange("m d c w -> m (d c w)").bitcast(F32)
@@ -200,10 +206,12 @@ def tile_mex_kernel(tc, x, offsets, out):
             state = {}
 
             def interleave():
-                nc.vector.tensor_copy(
-                    out=xi[bp][:, 134 * y0 : 134 * y1].rearrange("p (f q) -> p f q", q=2),
-                    in_=raw[(bp, ci)][:, :, 0 : W * rows].rearrange("p q f -> p f q"),
-                )
+                for r0, r1 in ((0, rows // 2 * 2), (rows // 2 * 2, rows)):
+                    if r1 > r0:
+                        nc.vector.tensor_copy(
+                            out=xi[bp][:, 134 * (y0 + r0) : 134 * (y0 + r1)].rearrange("p (f b) -> p f b", b=2),
+                            in_=raw[(bp, ci)][:, :, W * r0 : W * r1].rearrange("p b f -> p f b"),
+                        )
 
             def edges():
                 nc.vector.tensor_copy(
@@ -235,38 +243,37 @@ def tile_mex_kernel(tc, x, offsets, out):
                 return run
 
             def spread():
-                for b2 in range(2):
-                    nc.vector.tensor_scalar(
-                        out=pe[:, b2, 0:rows],
-                        in0=mask[:, 0:rows],
-                        scalar1=pm[:, b2, rows : rows + 1],
-                        scalar2=None,
-                        op0=ALU.mult,
-                    )
+                nc.vector.tensor_tensor(
+                    out=pe[:, :, 0:rows],
+                    in0=mask[:, 0:rows].unsqueeze(1).to_broadcast([P, 2, rows]),
+                    in1=pm[:, :, rows : rows + 1].to_broadcast([P, 2, rows]),
+                    op=ALU.mult,
+                )
 
             def shift_columns():
-                sh = ps_mb.tile([P, 3, 2, 24], F32, tag="mb", name="sh")
-                for i in range(3):
+                sh = ps_mb.tile([P, 4, 2, 24], F32, tag="mb", name="sh")
+                for i in range(4):
                     o = sh[:, i, :, :].rearrange("p b y -> p (b y)")
                     nc.tensor.matmul(
-                        out=o, lhsT=shift[:, i, :], rhs=pm[:].rearrange("p b y -> p (b y)"), start=True, stop=False
+                        out=o,
+                        lhsT=ident[:] if i == 0 else shift[:, i - 1, :],
+                        rhs=pm[:].rearrange("p b y -> p (b y)"),
+                        start=True,
+                        stop=(i == 0),
                     )
-                    nc.tensor.matmul(
-                        out=o, lhsT=edge[:, i, :], rhs=pe[:].rearrange("p b y -> p (b y)"), start=False, stop=True
-                    )
+                    if i:
+                        nc.tensor.matmul(
+                            out=o, lhsT=edge[:, i - 1, :], rhs=pe[:].rearrange("p b y -> p (b y)"), start=False, stop=True
+                        )
                 state["sh"] = sh
 
-            def shifted_max(i):
-                def run():
-                    last = pm[:, :, 0:rows] if i == 0 else state["w"][:, :, 0:rows]
-                    if i == 2:
-                        w = hm[bp][:, :, y0:y1]
-                    else:
-                        state["w"] = winp.tile([P, 2, 24], BF16, name="w%d" % i)
-                        w = state["w"][:, :, 0:rows]
-                    nc.vector.tensor_tensor(out=w, in0=state["sh"][:, i, :, 0:rows], in1=last, op=ALU.max)
-
-                return run
+            def row_max():
+                nc.vector.tensor_reduce(
+                    out=hm[bp][:, :, y0:y1],
+                    in_=state["sh"][:, :, :, 0:rows].rearrange("p i b y -> p b y i"),
+                    axis=mybir.AxisListType.X,
+                    op=ALU.max,
+                )
 
             def window1():
                 a1 = winp.tile([P, 134 * ROWS], BF16, name="a1")
@@ -352,7 +359,7 @@ def tile_mex_kernel(tc, x, offsets, out):
                     s1 = min(s0 + 8, rows + 1)
                     tasks = tasks + [turn_rows(s0, s1)] + gap + [reduce_rows(s0, s1)]
                 return (
-                    tasks + [spread] + gap + [shift_columns] + gap + [shifted_max(0), shifted_max(1), shifted_max(2)] + tail
+                    tasks + [spread] + gap + [shift_columns] + gap + [row_max] + tail
                 )
             return (
                 [interleave, window1, window2]
@@ -368,18 +375,23 @@ def tile_mex_kernel(tc, x, offsets, out):
 
         def make_m(bp, hb):
             made.append(0)
-            t = (ps_mb, ps_x1)[len(made) % 2].tile([P, 2, 4, P], BF16, tag=("mb", "x1")[len(made) % 2], name="m_bc")
-            for r in range(8):
-                h = 4 * hb + r % 4
-                nc.tensor.transpose(t[:, r // 4, r % 4, :], m_t[bp][:, r // 4, h : h + 1].to_broadcast([P, P]), ident[:])
+            pool, tag = ((ps_mb, "mb"), (ps_x1, "x1"))[len(made) % 2]
+            t = pool.tile([P, 2, 2, 4, WO], BF16, tag=tag, name="m_bc")
+            for q in range(2):
+                for h in range(4):
+                    nc.tensor.transpose(
+                        t[:, q, :, h, :], m_t[bp][:, q, 4 * hb + h : 4 * hb + h + 1].to_broadcast([P, P]), perm_w[:]
+                    )
             return t
 
         edge_tasks()
         first = [task for task in prepare_tasks(0, 0) if task]
         second = prepare_tasks(0, 1)
-        for task in first[:4] + [eb_max, eb_exp] + first[4:8] + second[:1] + first[8:] + second[1:3]:
+        third = prepare_tasks(0, 2)
+        ahead = 2 if NEW[0][1] else 3
+        for task in first[:4] + [eb_max, eb_exp] + first[4:8] + second[:1] + first[8:] + second[1:ahead] + third[:EARLY]:
             task()
-        background = second[3 + GAP :]
+        background = second[ahead + GAP :]
 
         sums = {}
         for bp in range(2):
@@ -410,16 +422,22 @@ def tile_mex_kernel(tc, x, offsets, out):
 
         def e1_rows(idx):
             bp, y = divmod(idx, YH)
-            for b2 in range(2):
-                e1 = e1p.tile([P, 256], F32, name="e1")
+            for q in range(2):
+                if q == 0 and y >= HH:
+                    e1_t[(bp, q, y)] = e1_t[(bp, 1, y - HH)]
+                    continue
+                if q == 1 and y < YH - HH:
+                    e1 = e1k.tile([P, 256], F32, name="e1_kept")
+                else:
+                    e1 = e1p.tile([P, 256], F32, name="e1")
                 nc.scalar.activation(
                     out=e1[:].rearrange("p (c d) -> p c d", d=4),
-                    in_=x1_t[idx // 2][:, idx % 2, :, 64 * b2 : 64 * b2 + 64].rearrange("p d c -> p c d"),
+                    in_=x1_t[idx // 2][:, idx % 2, :, 64 * q : 64 * q + 64].rearrange("p d c -> p c d"),
                     func=ACT.Exp,
-                    bias=neg_hm[bp][:, b2, y : y + 1],
+                    bias=neg_hm[bp][:, q, y : y + 1],
                     scale=1.0,
                 )
-                e1_t[(bp, b2, y)] = e1
+                e1_t[(bp, q, y)] = e1
 
         def mult(n):
             bp, b2, h = unit(n)
@@ -443,7 +461,7 @@ def tile_mex_kernel(tc, x, offsets, out):
             ex_t[n] = ex
 
         def t2(n):
-            tp = ps_tp.tile([P, 4, P], F32, name="tp")
+            tp = ps_tp.tile([P, 4, P], F32, tag="tp", name="tp")
             words = ex_t[n][:].bitcast(F32)
             for dh in range(4):
                 nc.tensor.transpose(tp[:, dh, :], words[:, P * dh : P * dh + P], ident_f[:])
@@ -469,10 +487,15 @@ def tile_mex_kernel(tc, x, offsets, out):
 
         def mx(gi, s):
             if s == 0:
-                acc_t[gi] = ps_acc.tile([P, 512], F32, name="acc")
+                if gi == 31:
+                    last_acc = ps_tp.tile([P, 4, P], F32, tag="tp", name="last_acc")
+                    acc_t[gi] = last_acc[:].rearrange("p d n -> p (d n)")
+                else:
+                    acc = ps_acc.tile([P, 512], F32, name="acc")
+                    acc_t[gi] = acc[:]
             codes, scales = q_t[gi]
             nc.tensor.matmul_mx(
-                out=acc_t[gi][:],
+                out=acc_t[gi],
                 lhsT=eb_codes[:, P * s : P * s + P].bitcast(FP8X4),
                 lhsT_scale=eb_scales[:, P * s : P * s + P],
                 rhs=codes[:, 512 * s : 512 * s + 512].bitcast(FP8X4),
@@ -484,10 +507,10 @@ def tile_mex_kernel(tc, x, offsets, out):
         def sum_view(gi):
             bp, g16 = divmod(gi, 16)
             hb, b2 = divmod(g16, 2)
-            return sums[bp][:, b2, :, 4 * hb : 4 * hb + 4, :].rearrange("m q h w -> m q (h w)")
+            return sums[bp][:, b2, :, 4 * hb : 4 * hb + 4, :].rearrange("m b h w -> m b (h w)")
 
         def acc_view(gi):
-            return acc_t[gi][:].rearrange("m (f q) -> m q f", q=2)
+            return acc_t[gi].rearrange("m (f b) -> m b f", b=2)
 
         def acc_copy(gi):
             nc.scalar.copy(out=sum_view(gi), in_=acc_view(gi))
@@ -496,29 +519,33 @@ def tile_mex_kernel(tc, x, offsets, out):
             nc.scalar.activation(out=sum_view(gi), in_=acc_view(gi), func=ACT.Ln)
 
         def store(bp, r0, rows):
-            for b2 in range(2):
-                for q in range(2):
+            for q in range(2):
+                for b2 in range(2):
                     nc.sync.dma_start(
                         out=out[2 * bp + b2, :, HH * q + r0 : HH * q + r0 + rows, :].rearrange("m h w -> m (h w)"),
-                        in_=sums[bp][:, b2, q, r0 : r0 + rows, :].rearrange("m h w -> m (h w)"),
+                        in_=sums[bp][:, q, b2, r0 : r0 + rows, :].rearrange("m h w -> m (h w)"),
                     )
 
-        to_log = []
+        copied = []
+        last_m = []
         logged = []
         to_finish = []
 
-        def log_sum(gi):
-            v = sum_view(gi)
+        def pair_view(pair):
+            bp, hb = divmod(pair, 8)
+            return sums[bp][:, :, :, 4 * hb : 4 * hb + 4, :].rearrange("m q b h w -> m (q b) (h w)")
+
+        def log_pair(pair):
+            v = pair_view(pair)
             nc.scalar.activation(out=v, in_=v, func=ACT.Ln)
 
-        def finish_group(gi, m_bc):
-            b2 = gi % 2
-            v = sum_view(gi)
+        def finish_pair(pair, m_bc, q0, q1):
+            v = pair_view(pair)[:, 2 * q0 : 2 * q1, :]
             nc.vector.scalar_tensor_tensor(
                 out=v,
                 in0=v,
                 scalar=cb[:, 0:1],
-                in1=m_bc[:, b2, :, :].rearrange("p h (w q) -> p q (h w)", q=2),
+                in1=m_bc[:].rearrange("p q b h w -> p (q b) (h w)")[:, 2 * q0 : 2 * q1, :],
                 op0=ALU.add,
                 op1=ALU.add,
             )
@@ -551,38 +578,46 @@ def tile_mex_kernel(tc, x, offsets, out):
             if (n - 3 - MLAG) % 4 == 0 and 0 <= n - 3 - MLAG < UNITS:
                 mx((n - 3 - MLAG) // 4, 0)
                 mx((n - 3 - MLAG) // 4, 1)
+            if n == UNITS + 7:
+                last_m.append(make_m(1, 7))
             while to_finish and to_finish[0][0] <= n:
-                due, gi, m_bc = to_finish.pop(0)
-                finish_group(gi, m_bc)
-                if gi % 4 == 3:
-                    store(gi // 16, 8 * (gi % 16 // 4), 8)
+                due, pair, m_bc = to_finish.pop(0)
+                if pair == 15:
+                    finish_pair(pair, m_bc, 0, 1)
+                    finish_pair(pair, m_bc, 1, 2)
+                else:
+                    finish_pair(pair, m_bc, 0, 2)
+                if pair % 2 == 1:
+                    store(pair // 8, 8 * (pair % 8 // 2), 8)
             if (n - 3 - ALAG) % 4 == 0 and 0 <= n - 3 - ALAG < UNITS:
                 gi = (n - 3 - ALAG) // 4
                 if e1_done < 2 * YH:
                     acc_copy(gi)
-                    to_log.append(gi)
+                    copied.append(gi)
                 else:
                     log_acc(gi)
                     logged.append(gi)
-                    logged.sort()
             if e1_done == 2 * YH:
-                some = to_log[: NLOG if n < UNITS else 99]
-                for gi in some:
-                    log_sum(gi)
-                logged = sorted(some + logged)
-                to_log = to_log[len(some) :]
-            pairs = 0
-            while len(logged) >= 2 and logged[0] % 2 == 0 and logged[1] == logged[0] + 1 and (pairs < FINN or n >= UNITS):
-                pairs += 1
-                m_bc = make_m(logged[0] // 16, logged[0] % 16 // 2)
-                for gi in logged[:2]:
-                    to_finish.append((n + DELAY, gi, m_bc))
-                logged = logged[2:]
+                if len(copied) == 1:
+                    v = sum_view(copied[0])
+                    nc.scalar.activation(out=v, in_=v, func=ACT.Ln)
+                    logged.append(copied.pop(0))
+                elif copied:
+                    log_pair(copied[0] // 2)
+                    logged.extend(copied[:2])
+                    copied = copied[2:]
+                logged.sort()
+            pairs = [gi // 2 for gi in logged if gi % 2 == 0 and gi + 1 in logged]
+            if pairs:
+                pair = pairs[0]
+                m_bc = last_m[0] if pair == 15 else make_m(pair // 8, pair % 8)
+                to_finish.append((n + DELAY, pair, m_bc))
+                logged = [gi for gi in logged if gi // 2 != pair]
             for key, at in PREPARE_AT.items():
                 if n == at:
-                    background = background + prepare_tasks(key[0], key[1])
+                    background = background + (third[EARLY:] if key == (0, 2) else prepare_tasks(key[0], key[1]))
             if n == EB_AT:
-                background = [eb_order, None, eb_turn, None, eb_copy, eb_quant] + background
+                background = [eb_turn, None, eb_copy, eb_quant] + background
             for i in range(RATE0 if n < -2 else RATE if n < RATE_TO else 1):
                 if background:
                     if background[0]:

from contextlib import ExitStack
import math

import concourse.bass as bass
import concourse.mybir as mybir
import concourse.tile as tile
from concourse.masks import make_identity

FLOPS = 2 * 128 * 1024 * 4 * 64 * 64

BF16 = mybir.dt.bfloat16
F32 = mybir.dt.float32
U32 = mybir.dt.uint32
U8 = mybir.dt.uint8
FP8X4 = mybir.dt.float8_e4m3fn_x4
ALU = mybir.AluOpType
ACT = mybir.ActivationFunctionType

P = 128
C = 64
W = 67
WO = 64
K = 1024
HH = 32
YH = HH + 3
UNITS = 128
LEAD = 9
LEAD0 = 5
QLAG = 5
MLAG = 8
ALAG = 9
GAP = 1
PER = 4
UOFF = 8
TLAG = 2
DELAY = 4
RATE0 = 6
RATE = 2
RATE_TO = 8
EARLY = 1
EB_AT = 4
SXM = 32
SX0 = 8
PREPARE_AT = {(0, 2): -2, (1, 0): 24, (1, 1): 46}
CHUNKS = ((0, 8), (8, 20), (20, YH))
CHUNKS1 = ((0, 14), (14, YH))
NEW = ((False, True, True), (True, True))
ROWS = 8
RAW = 1408


def tile_mex_kernel(tc, x, offsets, out):
    nc = tc.nc
    with ExitStack() as ctx:
        ctx.enter_context(tc.manual_schedule())
        const = ctx.enter_context(tc.tile_pool(name="const", bufs=1))
        rawp = ctx.enter_context(tc.tile_pool(name="raw", bufs=3))
        xip = ctx.enter_context(tc.tile_pool(name="xi", bufs=1))
        winp = ctx.enter_context(tc.tile_pool(name="win", bufs=1))
        e1k = ctx.enter_context(tc.tile_pool(name="e1k", bufs=6))
        e1p = ctx.enter_context(tc.tile_pool(name="e1", bufs=55))
        epool = ctx.enter_context(tc.tile_pool(name="ex", bufs=10))
        gpool = ctx.enter_context(tc.tile_pool(name="grouped", bufs=3))
        cpool = ctx.enter_context(tc.tile_pool(name="codes", bufs=2))
        spool = ctx.enter_context(tc.tile_pool(name="sums", bufs=1))
        ps_x1 = ctx.enter_context(tc.psum_pool(name="ps_x1", bufs=2))
        ps_tp = ctx.enter_context(tc.psum_pool(name="ps_tp", bufs=3))
        ps_acc = ctx.enter_context(tc.psum_pool(name="ps_acc", bufs=1))
        ps_mb = ctx.enter_context(tc.psum_pool(name="ps_mb", bufs=2))

        start = const.tile([P, 1], F32, name="start")
        nc.vector.memset(start[:], 0.0)
        nc.scalar.activation(out=start[:], in_=start[:], func=ACT.Exp)

        ident = const.tile([P, P], BF16, name="ident")
        make_identity(nc, ident[:])
        ident_f = const.tile([P, P], F32, name="ident_f")
        make_identity(nc, ident_f[:])
        perm = const.tile([P, P], BF16, name="perm")
        nc.vector.tensor_copy(
            out=perm[:].rearrange("p (x g i e) -> p x g i e", x=4, g=4, i=4, e=2),
            in_=ident[:].rearrange("p (x i g e) -> p x g i e", x=4, i=4, g=4, e=2),
        )

        perm_w = const.tile([P, P], BF16, name="perm_w")
        nc.vector.tensor_copy(
            out=perm_w[:].rearrange("p (b w) -> p b w", b=2), in_=ident[:].rearrange("p (w b) -> p b w", b=2)
        )

        raw = {}

        def load_chunk(bp, ci):
            y0, y1 = (CHUNKS, CHUNKS1)[bp][ci]
            raw[(bp, ci)] = rawp.tile([P, 2, RAW], BF16, name="raw")
            for b2 in range(2):
                for q in range(2):
                    nc.sync.dma_start(
                        out=raw[(bp, ci)][64 * q : 64 * q + 64, b2, 0 : W * (y1 - y0)],
                        in_=x[2 * bp + b2, :, HH * q + y0 : HH * q + y1, :].rearrange("c y z -> c (y z)"),
                    )

        load_chunk(0, 0)
        offs = const.tile([P, K], BF16, name="offs")
        nc.sync.dma_start(out=offs[:], in_=offsets[0].rearrange("m c i j -> m (c i j)"))
        load_chunk(0, 1)
        for bp, ci in [(0, c) for c in range(2, len(CHUNKS))] + [(1, c) for c in range(len(CHUNKS1))]:
            load_chunk(bp, ci)

        mb = const.tile([P, 1], F32, name="mb")
        neg_mb = const.tile([P, 1], F32, name="neg_mb")
        cb = const.tile([P, 1], F32, name="cb")
        eb_t = const.tile([P, 4, C, 4], BF16, name="eb_t")
        eb_g = const.tile([P, 2, P, 4], BF16, name="eb_g", align_bytes=64)
        eb_codes = const.tile([P, 2 * P], U32, name="eb_codes", align_bytes=64)
        eb_scales = const.tile([P, 2 * P], U8, name="eb_scales", align_bytes=64)

        eb = {}

        def eb_max():
            nc.vector.tensor_reduce(out=mb[:], in_=offs[:], axis=mybir.AxisListType.X, op=ALU.max)
            nc.vector.tensor_scalar(out=neg_mb[:], in0=mb[:], scalar1=-1.0, scalar2=None, op0=ALU.mult)
            nc.vector.tensor_scalar(out=cb[:], in0=mb[:], scalar1=-math.log(float(K)), scalar2=None, op0=ALU.add)

        def eb_exp():
            v = offs[:].rearrange("m (a i g e d w) -> m a g d i e w", a=2, i=4, g=4, e=2, d=4, w=4)
            for dh in range(4):
                for a in range(2):
                    for g in range(4):
                        c0 = 32 * a + 8 * g
                        nc.scalar.activation(
                            out=eb_t[:, dh, c0 : c0 + 8, :].rearrange("m (i e) w -> m i e w", e=2),
                            in_=v[:, a, g, dh, :, :, :],
                            func=ACT.Exp,
                            bias=neg_mb[:, 0:1],
                            scale=1.0,
                        )

        def eb_turn():
            eb_w = eb_t[:].rearrange("m d c w -> m (d c w)").bitcast(F32)
            eb["ps"] = ps_mb.tile([P, 4, P], F32, tag="mb", name="eb_ps")
            for dh in range(4):
                nc.tensor.transpose(eb["ps"][:, dh, :], eb_w[:, P * dh : P * dh + P], ident_f[:])

        def eb_copy():
            nc.vector.tensor_copy(
                out=eb_g[:].rearrange("q s m t -> q (s m t)").bitcast(F32).rearrange("q (s m u) -> q s m u", s=2, m=P, u=2),
                in_=eb["ps"][:].rearrange("q (s u) m -> q s m u", s=2, u=2),
            )

        def eb_quant():
            nc.vector.quantize_mx(
                out=eb_codes[:].bitcast(FP8X4),
                scales=eb_scales[:],
                in_=eb_g[:].rearrange("q s m t -> q (s m t)"),
            )

        xe = const.tile([P, P], BF16, name="xe")
        pm = const.tile([P, 2, 24], BF16, name="pm")
        pe = const.tile([P, 2, 24], BF16, name="pe")
        mask = const.tile([P, 24], BF16, name="mask")
        shift = const.tile([P, 3, P], BF16, name="shift")
        ends = const.tile([P, 3, P], BF16, name="ends")
        sixes = const.tile([P, P], BF16, name="sixes")
        edge = const.tile([P, 3, P], BF16, name="edge")
        for t in (xe, pm, pe, mask, shift, ends, sixes):
            nc.vector.memset(t[:], 0.0)

        def edge_tasks():
            nc.vector.tensor_reduce(
                out=mask[:, 0:21],
                in_=ident[:, 0:126].rearrange("p (y f) -> p y f", f=6),
                axis=mybir.AxisListType.X,
                op=ALU.max,
            )
            nc.scalar.copy(
                out=sixes[:, 0:126].rearrange("p (y f) -> p y f", f=6),
                in_=ident[:, 0:6].unsqueeze(1).to_broadcast([P, 21, 6]),
            )
            for i in range(3):
                n = 2 * (i + 1)
                nc.scalar.copy(out=shift[:, i, 0 : P - n], in_=ident[:, n:P])
                nc.scalar.copy(out=ends[:, i, P - n : P], in_=ident[:, 0:n])
            t = ps_mb.tile([P, 3, P], F32, tag="mb", name="edge_ps")
            for i in range(3):
                nc.tensor.matmul(out=t[:, i, :], lhsT=sixes[:], rhs=ends[:, i, :], start=True, stop=True)
            nc.scalar.copy(out=edge[:], in_=t[:])

        xi = {}
        hm = {}
        neg_hm = {}
        m_t = {}
        r_arg = {}
        r_t = {}
        for bp in range(2):
            xi[bp] = xip.tile([P, YH * W * 2], BF16, name="xi%d" % bp)
            hm[bp] = const.tile([P, 2, YH], BF16, name="hm%d" % bp)
            neg_hm[bp] = const.tile([P, 2, YH], F32, name="neg_hm%d" % bp)
            m_t[bp] = const.tile([P, 2, HH], BF16, name="m_t%d" % bp)
            r_arg[bp] = const.tile([P, 2, HH, 4], F32, name="r_arg%d" % bp)
            r_t[bp] = const.tile([P, 2, HH, 4], F32, name="r_t%d" % bp)

        def prepare_tasks(bp, ci):
            y0, y1 = (CHUNKS, CHUNKS1)[bp][ci]
            rows = y1 - y0
            h0, h1 = max(y0 - 3, 0), y1 - 3
            state = {}

            def interleave():
                for r0, r1 in ((0, rows // 2 * 2), (rows // 2 * 2, rows)):
                    if r1 > r0:
                        nc.vector.tensor_copy(
                            out=xi[bp][:, 134 * (y0 + r0) : 134 * (y0 + r1)].rearrange("p (f b) -> p f b", b=2),
                            in_=raw[(bp, ci)][:, :, W * r0 : W * r1].rearrange("p b f -> p f b"),
                        )

            def edges():
                nc.vector.tensor_copy(
                    out=xe[:, 0 : 6 * rows].rearrange("p (y f) -> p y f", f=6),
                    in_=xi[bp][:, 134 * y0 : 134 * y1].rearrange("p (y f) -> p y f", f=134)[:, :, 128:134],
                )

            def turn_rows(s0, s1):
                def run():
                    t = ps_mb.tile([P, 8, P], BF16, tag="mb", name="hm_ps")
                    for s in range(s0, s1):
                        f = 134 * (y0 + s)
                        nc.tensor.transpose(
                            t[:, s - s0, :], xi[bp][:, f : f + P] if s < rows else xe[:], ident[:]
                        )
                    state["t"] = t

                return run

            def reduce_rows(s0, s1):
                def run():
                    nc.vector.tensor_reduce(
                        out=pm[:, :, s0:s1].rearrange("p b y -> p y b"),
                        in_=state["t"][:, 0 : s1 - s0, :].rearrange("p y (b c) -> p y b c", b=2),
                        axis=mybir.AxisListType.X,
                        op=ALU.max,
                    )

                return run

            def spread():
                nc.vector.tensor_tensor(
                    out=pe[:, :, 0:rows],
                    in0=mask[:, 0:rows].unsqueeze(1).to_broadcast([P, 2, rows]),
                    in1=pm[:, :, rows : rows + 1].to_broadcast([P, 2, rows]),
                    op=ALU.mult,
                )

            def shift_columns():
                sh = ps_mb.tile([P, 4, 2, 24], F32, tag="mb", name="sh")
                for i in range(4):
                    o = sh[:, i, :, :].rearrange("p b y -> p (b y)")
                    nc.tensor.matmul(
                        out=o,
                        lhsT=ident[:] if i == 0 else shift[:, i - 1, :],
                        rhs=pm[:].rearrange("p b y -> p (b y)"),
                        start=True,
                        stop=(i == 0),
                    )
                    if i:
                        nc.tensor.matmul(
                            out=o, lhsT=edge[:, i - 1, :], rhs=pe[:].rearrange("p b y -> p (b y)"), start=False, stop=True
                        )
                state["sh"] = sh

            def row_max():
                nc.vector.tensor_reduce(
                    out=hm[bp][:, :, y0:y1],
                    in_=state["sh"][:, :, :, 0:rows].rearrange("p i b y -> p b y i"),
                    axis=mybir.AxisListType.X,
                    op=ALU.max,
                )

            def window1():
                a1 = winp.tile([P, 134 * ROWS], BF16, name="a1")
                n = 134 * rows - 2
                nc.vector.tensor_tensor(
                    out=a1[:, 0:n],
                    in0=xi[bp][:, 134 * y0 : 134 * y0 + n],
                    in1=xi[bp][:, 134 * y0 + 2 : 134 * y0 + 2 + n],
                    op=ALU.max,
                )
                state["a1"] = a1

            def window2():
                a2 = winp.tile([P, ROWS, P], BF16, name="a2")
                v = state["a1"][:, 0 : 134 * rows].rearrange("p (y f) -> p y f", y=rows)
                nc.vector.tensor_tensor(
                    out=a2[:, 0:rows, :], in0=v[:, :, 0:128], in1=v[:, :, 4:132], op=ALU.max
                )
                state["a2"] = a2

            def channel_rows(part):
                r0, r1 = (0, min(rows, 8)) if part == 0 else (8, rows)

                def turn():
                    t = ps_mb.tile([P, 8, P], BF16, tag="mb", name="hm_ps")
                    for r in range(r0, r1):
                        nc.tensor.transpose(t[:, r - r0, :], state["a2"][:, r, :], ident[:])
                    state["t"] = t

                def reduce():
                    nc.vector.tensor_reduce(
                        out=hm[bp][:, :, y0 + r0 : y0 + r1].rearrange("p b y -> p y b"),
                        in_=state["t"][:, 0 : r1 - r0, :].rearrange("p y (b c) -> p y b c", b=2),
                        axis=mybir.AxisListType.X,
                        op=ALU.max,
                    )

                return turn, reduce

            turn0, reduce0 = channel_rows(0)
            turn1, reduce1 = channel_rows(1) if rows > 8 else (None, None)

            def position_max():
                nc.vector.tensor_scalar(
                    out=neg_hm[bp][:, :, y0:y1], in0=hm[bp][:, :, y0:y1], scalar1=-1.0, scalar2=None, op0=ALU.mult
                )
                v1 = winp.tile([P, 2, 24], BF16, name="v1")
                state["v1"] = v1
                n = h1 - h0
                nc.vector.tensor_tensor(
                    out=v1[:, :, 0 : n + 2], in0=hm[bp][:, :, h0 : h1 + 2], in1=hm[bp][:, :, h0 + 1 : h1 + 3], op=ALU.max
                )

            def window_max():
                n = h1 - h0
                v1 = state["v1"]
                nc.vector.tensor_tensor(
                    out=m_t[bp][:, :, h0:h1], in0=v1[:, :, 0:n], in1=v1[:, :, 2 : n + 2], op=ALU.max
                )

            def differences():
                for dh in range(4):
                    nc.vector.tensor_tensor(
                        out=r_arg[bp][:, :, h0:h1, dh],
                        in0=hm[bp][:, :, h0 + dh : h1 + dh],
                        in1=m_t[bp][:, :, h0:h1],
                        op=ALU.subtract,
                    )

            def ratios():
                nc.scalar.activation(
                    out=r_t[bp][:, :, h0:h1, :].rearrange("p b h d -> p b (h d)"),
                    in_=r_arg[bp][:, :, h0:h1, :].rearrange("p b h d -> p b (h d)"),
                    func=ACT.Exp,
                )

            gap = [None] * GAP
            second = gap + [turn1] + gap + [reduce1] if rows > 8 else []
            tail = [position_max, window_max, differences] + gap + [ratios]
            if NEW[bp][ci]:
                tasks = [interleave, edges] + gap
                for s0 in range(0, rows + 1, 8):
                    s1 = min(s0 + 8, rows + 1)
                    tasks = tasks + [turn_rows(s0, s1)] + gap + [reduce_rows(s0, s1)]
                return (
                    tasks + [spread] + gap + [shift_columns] + gap + [row_max] + tail
                )
            return (
                [interleave, window1, window2]
                + gap
                + [turn0]
                + gap
                + [reduce0]
                + second
                + tail
            )

        made = []

        def make_m(bp, hb):
            made.append(0)
            pool, tag = ((ps_mb, "mb"), (ps_x1, "x1"))[len(made) % 2]
            t = pool.tile([P, 2, 2, 4, WO], BF16, tag=tag, name="m_bc")
            for q in range(2):
                for h in range(4):
                    nc.tensor.transpose(
                        t[:, q, :, h, :], m_t[bp][:, q, 4 * hb + h : 4 * hb + h + 1].to_broadcast([P, P]), perm_w[:]
                    )
            return t

        edge_tasks()
        first = [task for task in prepare_tasks(0, 0) if task]
        second = prepare_tasks(0, 1)
        third = prepare_tasks(0, 2)
        ahead = 2 if NEW[0][1] else 3
        for task in first[:4] + [eb_max, eb_exp] + first[4:8] + second[:1] + first[8:] + second[1:ahead] + third[:EARLY]:
            task()
        background = second[ahead + GAP :]

        sums = {}
        for bp in range(2):
            sums[bp] = spool.tile([P, 2, 2, HH, WO], F32, name="sum%d" % bp)
        e1_t = {}
        ex_t = {}
        tp_t = {}
        g_t = {}
        q_t = {}
        acc_t = {}

        def unit(n):
            bp, r = divmod(n, 64)
            hb, r = divmod(r, 8)
            b2, j = divmod(r, 4)
            return bp, b2, 4 * hb + j

        x1_t = {}

        def t1(i):
            x1 = ps_x1.tile([P, 2, 4, P], BF16, tag="x1", name="x1")
            for k in range(2):
                bp, y = divmod(2 * i + k, YH)
                for dw in range(4):
                    f = 134 * y + 2 * dw
                    nc.tensor.transpose(x1[:, k, dw, :], xi[bp][:, f : f + P], perm[:])
            x1_t[i] = x1

        def e1_rows(idx):
            bp, y = divmod(idx, YH)
            for q in range(2):
                if q == 0 and y >= HH:
                    e1_t[(bp, q, y)] = e1_t[(bp, 1, y - HH)]
                    continue
                if q == 1 and y < YH - HH:
                    e1 = e1k.tile([P, 256], F32, name="e1_kept")
                else:
                    e1 = e1p.tile([P, 256], F32, name="e1")
                nc.scalar.activation(
                    out=e1[:].rearrange("p (c d) -> p c d", d=4),
                    in_=x1_t[idx // 2][:, idx % 2, :, 64 * q : 64 * q + 64].rearrange("p d c -> p c d"),
                    func=ACT.Exp,
                    bias=neg_hm[bp][:, q, y : y + 1],
                    scale=1.0,
                )
                e1_t[(bp, q, y)] = e1

        def mult(n):
            bp, b2, h = unit(n)
            ex = epool.tile([P, K], BF16, name="ex")
            for dh in range(4):
                if dh == 3 and (n % SXM == 3 or n < SX0):
                    nc.scalar.activation(
                        out=ex[:, 256 * dh : 256 * dh + 256],
                        in_=e1_t[(bp, b2, h + dh)][:],
                        func=ACT.Copy,
                        scale=r_t[bp][:, b2, h, dh : dh + 1],
                    )
                else:
                    nc.vector.tensor_scalar(
                        out=ex[:, 256 * dh : 256 * dh + 256],
                        in0=e1_t[(bp, b2, h + dh)][:],
                        scalar1=r_t[bp][:, b2, h, dh : dh + 1],
                        scalar2=None,
                        op0=ALU.mult,
                    )
            ex_t[n] = ex

        def t2(n):
            tp = ps_tp.tile([P, 4, P], F32, tag="tp", name="tp")
            words = ex_t[n][:].bitcast(F32)
            for dh in range(4):
                nc.tensor.transpose(tp[:, dh, :], words[:, P * dh : P * dh + P], ident_f[:])
            tp_t[n] = tp

        def cpo(n):
            gi, j4 = divmod(n, 4)
            if j4 == 0:
                g_t[gi] = gpool.tile([P, 2, 2048], BF16, name="g", align_bytes=64)
            gw = g_t[gi][:].rearrange("q s k -> q (s k)").bitcast(F32).rearrange("q (s k) -> q s k", s=2)
            nc.scalar.copy(
                out=gw[:, :, 256 * j4 : 256 * j4 + 256].rearrange("q s (n u) -> q s n u", u=2),
                in_=tp_t[n][:].rearrange("q (s u) n -> q s n u", s=2, u=2),
            )

        def quant(gi):
            codes = cpool.tile([P, 1024], U32, name="codes", align_bytes=64)
            scales = cpool.tile([P, 1024], U8, name="scales", align_bytes=64)
            nc.vector.quantize_mx(
                out=codes[:].bitcast(FP8X4), scales=scales[:], in_=g_t[gi][:].rearrange("q s k -> q (s k)")
            )
            q_t[gi] = (codes, scales)

        def mx(gi, s):
            if s == 0:
                if gi == 31:
                    last_acc = ps_tp.tile([P, 4, P], F32, tag="tp", name="last_acc")
                    acc_t[gi] = last_acc[:].rearrange("p d n -> p (d n)")
                else:
                    acc = ps_acc.tile([P, 512], F32, name="acc")
                    acc_t[gi] = acc[:]
            codes, scales = q_t[gi]
            nc.tensor.matmul_mx(
                out=acc_t[gi],
                lhsT=eb_codes[:, P * s : P * s + P].bitcast(FP8X4),
                lhsT_scale=eb_scales[:, P * s : P * s + P],
                rhs=codes[:, 512 * s : 512 * s + 512].bitcast(FP8X4),
                rhs_scale=scales[:, 512 * s : 512 * s + 512],
                start=(s == 0),
                stop=(s == 1),
            )

        def sum_view(gi):
            bp, g16 = divmod(gi, 16)
            hb, b2 = divmod(g16, 2)
            return sums[bp][:, b2, :, 4 * hb : 4 * hb + 4, :].rearrange("m b h w -> m b (h w)")

        def acc_view(gi):
            return acc_t[gi].rearrange("m (f b) -> m b f", b=2)

        def acc_copy(gi):
            nc.scalar.copy(out=sum_view(gi), in_=acc_view(gi))

        def log_acc(gi):
            nc.scalar.activation(out=sum_view(gi), in_=acc_view(gi), func=ACT.Ln)

        def store(bp, r0, rows):
            for q in range(2):
                for b2 in range(2):
                    nc.sync.dma_start(
                        out=out[2 * bp + b2, :, HH * q + r0 : HH * q + r0 + rows, :].rearrange("m h w -> m (h w)"),
                        in_=sums[bp][:, q, b2, r0 : r0 + rows, :].rearrange("m h w -> m (h w)"),
                    )

        copied = []
        last_m = []
        logged = []
        to_finish = []

        def pair_view(pair):
            bp, hb = divmod(pair, 8)
            return sums[bp][:, :, :, 4 * hb : 4 * hb + 4, :].rearrange("m q b h w -> m (q b) (h w)")

        def log_pair(pair):
            v = pair_view(pair)
            nc.scalar.activation(out=v, in_=v, func=ACT.Ln)

        def finish_pair(pair, m_bc, q0, q1):
            v = pair_view(pair)[:, 2 * q0 : 2 * q1, :]
            nc.vector.scalar_tensor_tensor(
                out=v,
                in0=v,
                scalar=cb[:, 0:1],
                in1=m_bc[:].rearrange("p q b h w -> p (q b) (h w)")[:, 2 * q0 : 2 * q1, :],
                op0=ALU.add,
                op1=ALU.add,
            )

        freed = []
        t1_done = 0
        e1_done = 0
        mults = 0
        for n in range(-LEAD0, UNITS + 6 + ALAG):
            u = n + min(LEAD, LEAD0 + max(n, 0) // 2)
            target = min(2 * YH, 5 + u, 8 + 2 * ((u + UOFF) // PER))
            freed.append(e1_done // 2)
            while e1_done < target:
                while t1_done < min(e1_done // 2 + 1, YH):
                    t1(t1_done)
                    t1_done += 1
                e1_rows(e1_done)
                e1_done += 1
            if t1_done < YH and len(freed) > TLAG and t1_done <= freed[-1 - TLAG] + 1:
                t1(t1_done)
                t1_done += 1
            if 0 <= n < UNITS:
                t2(n)
                cpo(n)
            if (n - 3 - QLAG) % 4 == 0 and 0 <= n - 3 - QLAG < UNITS:
                quant((n - 3 - QLAG) // 4)
            while mults < min(UNITS, u + 1):
                mult(mults)
                mults += 1
            if (n - 3 - MLAG) % 4 == 0 and 0 <= n - 3 - MLAG < UNITS:
                mx((n - 3 - MLAG) // 4, 0)
                mx((n - 3 - MLAG) // 4, 1)
            if n == UNITS + 7:
                last_m.append(make_m(1, 7))
            while to_finish and to_finish[0][0] <= n:
                due, pair, m_bc = to_finish.pop(0)
                if pair == 15:
                    finish_pair(pair, m_bc, 0, 1)
                    finish_pair(pair, m_bc, 1, 2)
                else:
                    finish_pair(pair, m_bc, 0, 2)
                if pair % 2 == 1:
                    store(pair // 8, 8 * (pair % 8 // 2), 8)
            if (n - 3 - ALAG) % 4 == 0 and 0 <= n - 3 - ALAG < UNITS:
                gi = (n - 3 - ALAG) // 4
                if e1_done < 2 * YH:
                    acc_copy(gi)
                    copied.append(gi)
                else:
                    log_acc(gi)
                    logged.append(gi)
            if e1_done == 2 * YH:
                if len(copied) == 1:
                    v = sum_view(copied[0])
                    nc.scalar.activation(out=v, in_=v, func=ACT.Ln)
                    logged.append(copied.pop(0))
                elif copied:
                    log_pair(copied[0] // 2)
                    logged.extend(copied[:2])
                    copied = copied[2:]
                logged.sort()
            pairs = [gi // 2 for gi in logged if gi % 2 == 0 and gi + 1 in logged]
            if pairs:
                pair = pairs[0]
                m_bc = last_m[0] if pair == 15 else make_m(pair // 8, pair % 8)
                to_finish.append((n + DELAY, pair, m_bc))
                logged = [gi for gi in logged if gi // 2 != pair]
            for key, at in PREPARE_AT.items():
                if n == at:
                    background = background + (third[EARLY:] if key == (0, 2) else prepare_tasks(key[0], key[1]))
            if n == EB_AT:
                background = [eb_turn, None, eb_copy, eb_quant] + background
            for i in range(RATE0 if n < -2 else RATE if n < RATE_TO else 1):
                if background:
                    if background[0]:
                        background[0]()
                    background = background[1:]
